import numpy as np
import ml_dtypes


def mxq(x, axis, fmt="e4m3"):
    dtype, down = {"e4m3": (ml_dtypes.float8_e4m3fn, 7), "e5m2": (ml_dtypes.float8_e5m2, 14)}[fmt]
    v = np.moveaxis(np.asarray(x, np.float32).astype(ml_dtypes.bfloat16).astype(np.float64), axis, -1)
    blocks = v.reshape(v.shape[:-1] + (-1, 32))
    amax = np.abs(blocks).max(-1, keepdims=True)
    byte = np.maximum(np.where(amax > 0, np.frexp(amax)[1] - 1 + 127, 0) - down, 1)
    scale = np.exp2(byte - 127.0)
    codes = (blocks / scale).astype(np.float32).astype(dtype).astype(np.float64)
    return np.moveaxis((codes * scale).reshape(v.shape), -1, axis)


WIDE = False


def mx_kscale(k):
    if not WIDE:
        return np.ones(k)
    levels = np.array([10, -10, 5, -5, 0])
    a = np.random.permutation(np.resize(levels, k // 512 * 4)).reshape(k // 512, 4)
    idx = np.arange(k)
    return np.exp2(a[idx // 512, idx % 128 // 32])


BF16 = ml_dtypes.bfloat16


def bf(x):
    return np.asarray(x, np.float32).astype(BF16)


def f64(x):
    return np.asarray(x).astype(np.float64)


B, CIN, COUT, H, L = 128, 32, 128, 512, 1024
G = 1.0 / np.sqrt(CIN * L)


def setup_inputs():
    s = mx_kscale(H)
    return {"x": bf(np.random.standard_normal((B, CIN, L))),
            "h_sine": bf(np.sin(np.random.uniform(-np.pi, np.pi, (L, H))) * s),
            "w3": bf(np.random.standard_normal((COUT * CIN, H)) * 1.4 * G / np.sqrt(H) / s[None, :]),
            "b3": bf(np.random.standard_normal(COUT * CIN) * 0.3 * G),
            "bias": bf(np.random.standard_normal(COUT) * 0.2)}


def reference(x, h_sine, w3, b3, bias):
    k = (mxq(f64(h_sine), 1, "e4m3") @ mxq(f64(w3), 1, "e4m3").T) + f64(b3)
    kernel = k.T.reshape(COUT, CIN * L)
    out = (mxq(f64(x).reshape(B, CIN * L), 1, "e4m3") @ mxq(kernel, 1, "e4m3").T) + f64(bias)
    return out[:, :, None]

@@ -1,0 +1,235 @@
+from contextlib import ExitStack
+
+import concourse.mybir as mybir
+from concourse.masks import make_identity
+
+F32 = mybir.dt.float32
+BF16 = mybir.dt.bfloat16
+U32 = mybir.dt.uint32
+U8 = mybir.dt.uint8
+FP8X4 = mybir.dt.float8_e4m3fn_x4
+ADD = mybir.AluOpType.add
+
+P = 128
+CIN = 32
+ROUNDS = 16
+FLOPS = 2 * 1024 * 4096 * 512 + 2 * 128 * 128 * 32768
+
+GP = False
+ORDER = [3, 0, 2, 1] if GP else [0, 2, 1, 3]
+
+
+def tile_ckconv_pa_kernel(tc, x, h_sine, w3, b3, bias, out):
+    nc = tc.nc
+    with ExitStack() as ctx:
+        ctx.enter_context(tc.manual_schedule())
+        const = ctx.enter_context(tc.tile_pool(name="const", bufs=1))
+        loads = ctx.enter_context(tc.tile_pool(name="loads", bufs=1))
+        grp = ctx.enter_context(tc.tile_pool(name="grp", bufs=3))
+        cod = ctx.enter_context(tc.tile_pool(name="cod", bufs=3))
+        tps = ctx.enter_context(tc.psum_pool(name="ps_t", bufs=3))
+        kps = ctx.enter_context(tc.psum_pool(name="ps_k", bufs=4))
+        aps = ctx.enter_context(tc.psum_pool(name="ps_a", bufs=1))
+
+        b3T = const.tile([P, CIN], BF16, name="b3T")
+        nc.sync.dma_start(out=b3T[:], in_=b3.rearrange("(o i) -> o i", i=CIN))
+        hs_view = h_sine.rearrange("(g u p e) h -> g p u (e h)", g=2, u=2, p=P, e=2)
+        w_view = w3.rearrange("(o i) h -> o (i h)", i=CIN)
+        x_view = x.rearrange("b i l -> b (i l)")
+        hs_sb = [const.tile([P, 2, 1024], BF16, name="hs_sb%d" % g) for g in range(2)]
+        w_sb = [loads.tile([P, 1024], BF16, name="w_sb%d" % r) for r in range(ROUNDS)]
+        x_sb = [loads.tile([P, 2048], BF16, name="x_sb%d" % r) for r in range(ROUNDS)]
+
+        def load_w(r):
+            nc.sync.dma_start(out=w_sb[r][:], in_=w_view[:, 1024 * r : 1024 * (r + 1)])
+
+        def load_x(r):
+            nc.sync.dma_start(out=x_sb[r][:], in_=x_view[:, 2048 * r : 2048 * (r + 1)])
+
+        nc.sync.dma_start(out=hs_sb[0][:], in_=hs_view[0])
+        load_w(0)
+        nc.sync.dma_start(out=hs_sb[1][:], in_=hs_view[1])
+        load_w(1)
+        load_w(2)
+        for r in range(ROUNDS):
+            load_x(r)
+            if r + 3 < ROUNDS:
+                load_w(r + 3)
+        bias_bc = const.tile([P, P], BF16, name="bias_bc")
+        nc.sync.dma_start(out=bias_bc[:], in_=bias.partition_broadcast(P))
+
+        ident_f = const.tile([P, P], F32, name="ident_f")
+        make_identity(nc, ident_f[:])
+        ident_b = const.tile([P, P], BF16, name="ident_b")
+        make_identity(nc, ident_b[:])
+
+        b3bc = const.tile([P, CIN, P], BF16, name="b3bc")
+        hs_codes = const.tile([P, 1024], U32, name="hs_codes", align_bytes=64)
+        hs_scales = const.tile([P, 1024], U8, name="hs_scales", align_bytes=64)
+        acc = aps.tile([P, P], F32, name="acc")
+
+        def leave(engine, dest, src):
+            if engine == "v":
+                nc.vector.tensor_copy(out=dest, in_=src)
+            else:
+                nc.scalar.copy(out=dest, in_=src)
+
+        def flip(units, dest, engine):
+            bank = tps.tile([P, 2, 2, P], F32, name="tbank", tag="tbank")
+            for n, (src, col) in enumerate(units):
+                for u in range(2):
+                    nc.tensor.transpose(bank[:, n, u, :], src[:, col + P * u : col + P * (u + 1)], ident_f[:])
+            leave(engine, dest.rearrange("p (n r u) -> p n r u", n=2, u=2), bank[:].rearrange("p n u r -> p n r u"))
+
+        def spread_b3(jb, engine):
+            bank = tps.tile([P, 4, P], F32, name="bbank", tag="tbank")
+            for q in range(4):
+                c = 4 * jb + q
+                nc.tensor.matmul(out=bank[:, q, :], lhsT=b3T[:, c : c + 1].to_broadcast([P, P]), rhs=ident_b[:], start=True, stop=True)
+            leave(engine, b3bc[:, 4 * jb : 4 * jb + 4, :], bank[:])
+
+        gh = {}
+
+        def flip_h(g, half, engine):
+            if half == 0:
+                gh[g] = grp.tile([P, 2048], BF16, name="gh", tag="gh", bufs=2, align_bytes=64)
+            src = hs_sb[g][:].rearrange("p u c -> p (u c)").bitcast(F32)
+            flip([(src, 256 * (2 * half)), (src, 256 * (2 * half + 1))], gh[g][:].bitcast(F32)[:, 512 * half : 512 * (half + 1)], engine)
+
+        def quant_h(g):
+            nc.vector.quantize_mx(out=hs_codes[:, 512 * g : 512 * (g + 1)].bitcast(FP8X4), scales=hs_scales[:, 512 * g : 512 * (g + 1)], in_=gh[g][:])
+
+        gw, wc, ws = {}, {}, {}
+
+        def flip_w(r):
+            gw[r] = grp.tile([P, 1024], BF16, name="gw", tag="gw", align_bytes=64)
+            src = w_sb[r][:].bitcast(F32)
+            flip([(src, 0), (src, 256)], gw[r][:].bitcast(F32), "s")
+
+        def quant_w(r):
+            wc[r] = cod.tile([P, 256], U32, name="wc", tag="wc", align_bytes=64)
+            ws[r] = cod.tile([P, 256], U8, name="ws", tag="ws", align_bytes=64)
+            nc.vector.quantize_mx(out=wc[r][:].bitcast(FP8X4), scales=ws[r][:], in_=gw[r][:])
+
+        gx, xc, xs = {}, {}, {}
+
+        def flip_x(r):
+            gx[r] = grp.tile([P, 2048], BF16, name="gx", tag="gx", align_bytes=64)
+            src = x_sb[r][:].bitcast(F32)
+            for n in range(2):
+                flip([(src, 512 * n), (src, 512 * n + 256)], gx[r][:].bitcast(F32)[:, 512 * n : 512 * (n + 1)], "s")
+
+        def quant_x(r):
+            xc[r] = cod.tile([P, 512], U32, name="xc", tag="xc", bufs=4, align_bytes=64)
+            xs[r] = cod.tile([P, 512], U8, name="xs", tag="xs", bufs=4, align_bytes=64)
+            nc.vector.quantize_mx(out=xc[r][:].bitcast(FP8X4), scales=xs[r][:], in_=gx[r][:])
+
+        kb, gk, kc, ks, kf = {}, {}, {}, {}, {}
+
+        def stage1(r, j):
+            n, g = j // 2, j % 2
+            kb[r, j] = kps.tile([P, 4, P], F32, name="kbank", tag="kbank")
+            for t in range(4):
+                c = P * (4 * g + t)
+                nc.tensor.matmul_mx(
+                    out=kb[r, j][:, t, :],
+                    lhsT=hs_codes[:, c : c + P].bitcast(FP8X4),
+                    lhsT_scale=hs_scales[:, c : c + P],
+                    rhs=wc[r][:, P * n : P * (n + 1)].bitcast(FP8X4),
+                    rhs_scale=ws[r][:, P * n : P * (n + 1)],
+                    start=True,
+                    stop=True,
+                )
+
+        def b3_of(r, j):
+            return b3bc[:, 2 * r + j // 2, :].unsqueeze(2).to_broadcast([P, P, 4])
+
+        def new_gk(r):
+            gk[r] = grp.tile([P, 4, P, 4], BF16, name="gk", tag="gk", bufs=(1 if GP else 2), align_bytes=64)
+
+        def add_b3(r, j):
+            nc.vector.tensor_tensor(out=gk[r][:, j, :, :], in0=kb[r, j][:].rearrange("p t o -> p o t"), in1=b3_of(r, j), op=ADD)
+
+        def side_exit(r, j):
+            kf[r] = grp.tile([P, P, 4], F32, name="kf", tag="kf", bufs=2)
+            nc.scalar.copy(out=kf[r][:], in_=kb[r, j][:].rearrange("p t o -> p o t"))
+
+        def side_add(r, j):
+            nc.gpsimd.tensor_tensor(out=gk[r][:, j, :, :], in0=kf[r][:], in1=b3_of(r, j), op=ADD)
+
+        def quant_k(r):
+            kc[r] = cod.tile([P, 512], U32, name="kc", tag="kc", align_bytes=64)
+            ks[r] = cod.tile([P, 512], U8, name="ks", tag="ks", align_bytes=64)
+            nc.vector.quantize_mx(out=kc[r][:].bitcast(FP8X4), scales=ks[r][:], in_=gk[r][:].rearrange("p j o t -> p (j o t)"))
+
+        def stage2(r):
+            for j in range(4):
+                cols = slice(P * j, P * (j + 1))
+                nc.tensor.matmul_mx(
+                    out=acc[:],
+                    lhsT=xc[r][:, cols].bitcast(FP8X4),
+                    lhsT_scale=xs[r][:, cols],
+                    rhs=kc[r][:, cols].bitcast(FP8X4),
+                    rhs_scale=ks[r][:, cols],
+                    start=(r == 0 and j == 0),
+                    stop=(r == ROUNDS - 1 and j == 3),
+                )
+
+        def stage1_round(r, j):
+            stage1(r, j)
+            if GP and j == 3:
+                side_exit(r, j)
+
+        spread_b3(0, "v")
+        flip_h(0, 0, "s")
+        flip_h(0, 1, "v")
+        quant_h(0)
+        flip_w(0)
+        quant_w(0)
+        flip_h(1, 0, "s")
+        flip_h(1, 1, "v")
+        quant_h(1)
+        flip_w(1)
+        for j in ORDER:
+            stage1_round(0, j)
+        new_gk(0)
+        if GP:
+            side_add(0, 3)
+        flip_w(2)
+        flip_x(0)
+
+        for s in range(ROUNDS):
+            nxt = s + 1 < ROUNDS
+            if s == 0:
+                for j in ORDER:
+                    if not (GP and j == 3):
+                        add_b3(s, j)
+                quant_w(1)
+                for j in ORDER:
+                    stage1_round(1, j)
+            else:
+                for j in ORDER:
+                    if not (GP and j == 3):
+                        add_b3(s, j)
+                    if nxt:
+                        stage1_round(s + 1, j)
+                stage2(s - 1)
+            quant_x(s)
+            if s + 2 < ROUNDS:
+                quant_w(s + 2)
+            quant_k(s)
+            if nxt:
+                new_gk(s + 1)
+                if GP:
+                    side_add(s + 1, 3)
+            if s + 3 < ROUNDS:
+                flip_w(s + 3)
+            if nxt:
+                flip_x(s + 1)
+            if s % 2 == 0 and s // 2 + 1 < CIN // 4:
+                spread_b3(s // 2 + 1, "s")
+        stage2(ROUNDS - 1)
+
+        res = const.tile([P, P], F32, name="res")
+        nc.vector.tensor_tensor(out=res[:], in0=acc[:], in1=bias_bc[:], op=ADD)
+        nc.sync.dma_start(out=out.rearrange("b o z -> b (o z)"), in_=res[:])

@@ -15,7 +15,7 @@ CIN = 32
 ROUNDS = 16
 FLOPS = 2 * 1024 * 4096 * 512 + 2 * 128 * 128 * 32768
 
-GP = False
+GP = True
 ORDER = [3, 0, 2, 1] if GP else [0, 2, 1, 3]
 
 

@@ -15,8 +15,8 @@ CIN = 32
 ROUNDS = 16
 FLOPS = 2 * 1024 * 4096 * 512 + 2 * 128 * 128 * 32768
 
-GP = True
-ORDER = [3, 0, 2, 1] if GP else [0, 2, 1, 3]
+SIDE = 3
+MAIN = [0, 1, 2]
 
 
 def tile_ckconv_pa_kernel(tc, x, h_sine, w3, b3, bias, out):
@@ -50,18 +50,17 @@ def tile_ckconv_pa_kernel(tc, x, h_sine, w3, b3, bias, out):
         load_w(0)
         nc.sync.dma_start(out=hs_sb[1][:], in_=hs_view[1])
         load_w(1)
-        load_w(2)
         for r in range(ROUNDS):
             load_x(r)
-            if r + 3 < ROUNDS:
-                load_w(r + 3)
+            if r + 2 < ROUNDS:
+                load_w(r + 2)
         bias_bc = const.tile([P, P], BF16, name="bias_bc")
         nc.sync.dma_start(out=bias_bc[:], in_=bias.partition_broadcast(P))
 
         ident_f = const.tile([P, P], F32, name="ident_f")
-        make_identity(nc, ident_f[:])
         ident_b = const.tile([P, P], BF16, name="ident_b")
         make_identity(nc, ident_b[:])
+        make_identity(nc, ident_f[:])
 
         b3bc = const.tile([P, CIN, P], BF16, name="b3bc")
         hs_codes = const.tile([P, 1024], U32, name="hs_codes", align_bytes=64)
@@ -96,8 +95,11 @@ def tile_ckconv_pa_kernel(tc, x, h_sine, w3, b3, bias, out):
             src = hs_sb[g][:].rearrange("p u c -> p (u c)").bitcast(F32)
             flip([(src, 256 * (2 * half)), (src, 256 * (2 * half + 1))], gh[g][:].bitcast(F32)[:, 512 * half : 512 * (half + 1)], engine)
 
+        def quant(codes, scales, src):
+            nc.vector.quantize_mx(out=codes.bitcast(FP8X4), scales=scales, in_=src)
+
         def quant_h(g):
-            nc.vector.quantize_mx(out=hs_codes[:, 512 * g : 512 * (g + 1)].bitcast(FP8X4), scales=hs_scales[:, 512 * g : 512 * (g + 1)], in_=gh[g][:])
+            quant(hs_codes[:, 512 * g : 512 * (g + 1)], hs_scales[:, 512 * g : 512 * (g + 1)], gh[g][:])
 
         gw, wc, ws = {}, {}, {}
 
@@ -109,30 +111,30 @@ def tile_ckconv_pa_kernel(tc, x, h_sine, w3, b3, bias, out):
         def quant_w(r):
             wc[r] = cod.tile([P, 256], U32, name="wc", tag="wc", align_bytes=64)
             ws[r] = cod.tile([P, 256], U8, name="ws", tag="ws", align_bytes=64)
-            nc.vector.quantize_mx(out=wc[r][:].bitcast(FP8X4), scales=ws[r][:], in_=gw[r][:])
+            quant(wc[r][:], ws[r][:], gw[r][:])
 
         gx, xc, xs = {}, {}, {}
 
         def flip_x(r):
             gx[r] = grp.tile([P, 2048], BF16, name="gx", tag="gx", align_bytes=64)
             src = x_sb[r][:].bitcast(F32)
-            for n in range(2):
-                flip([(src, 512 * n), (src, 512 * n + 256)], gx[r][:].bitcast(F32)[:, 512 * n : 512 * (n + 1)], "s")
+            for g in range(2):
+                flip([(src, 256 * g), (src, 512 + 256 * g)], gx[r][:].bitcast(F32)[:, 512 * g : 512 * (g + 1)], "s")
 
         def quant_x(r):
             xc[r] = cod.tile([P, 512], U32, name="xc", tag="xc", bufs=4, align_bytes=64)
             xs[r] = cod.tile([P, 512], U8, name="xs", tag="xs", bufs=4, align_bytes=64)
-            nc.vector.quantize_mx(out=xc[r][:].bitcast(FP8X4), scales=xs[r][:], in_=gx[r][:])
+            quant(xc[r][:], xs[r][:], gx[r][:])
 
-        kb, gk, kc, ks, kf = {}, {}, {}, {}, {}
+        kb, gk, gs, kc, ks, kf = {}, {}, {}, {}, {}, {}
 
-        def stage1(r, j):
-            n, g = j // 2, j % 2
-            kb[r, j] = kps.tile([P, 4, P], F32, name="kbank", tag="kbank")
+        def stage1(r, q):
+            g, n = q // 2, q % 2
+            kb[r, q] = kps.tile([P, 4, P], F32, name="kbank", tag="kbank")
             for t in range(4):
                 c = P * (4 * g + t)
                 nc.tensor.matmul_mx(
-                    out=kb[r, j][:, t, :],
+                    out=kb[r, q][:, t, :],
                     lhsT=hs_codes[:, c : c + P].bitcast(FP8X4),
                     lhsT_scale=hs_scales[:, c : c + P],
                     rhs=wc[r][:, P * n : P * (n + 1)].bitcast(FP8X4),
@@ -140,47 +142,48 @@ def tile_ckconv_pa_kernel(tc, x, h_sine, w3, b3, bias, out):
                     start=True,
                     stop=True,
                 )
+            if q == SIDE:
+                kf[r] = grp.tile([P, P, 4], F32, name="kf", tag="kf", bufs=2)
+                nc.scalar.copy(out=kf[r][:], in_=kb[r, q][:].rearrange("p t o -> p o t"))
 
-        def b3_of(r, j):
-            return b3bc[:, 2 * r + j // 2, :].unsqueeze(2).to_broadcast([P, P, 4])
+        def b3_of(r, q):
+            return b3bc[:, 2 * r + q % 2, :].unsqueeze(2).to_broadcast([P, P, 4])
 
-        def new_gk(r):
-            gk[r] = grp.tile([P, 4, P, 4], BF16, name="gk", tag="gk", bufs=(1 if GP else 2), align_bytes=64)
+        def add_b3(r, q):
+            if q == 0:
+                gk[r] = grp.tile([P, 3, P, 4], BF16, name="gk", tag="gk", bufs=2, align_bytes=64)
+            nc.vector.tensor_tensor(out=gk[r][:, q, :, :], in0=kb[r, q][:].rearrange("p t o -> p o t"), in1=b3_of(r, q), op=ADD)
 
-        def add_b3(r, j):
-            nc.vector.tensor_tensor(out=gk[r][:, j, :, :], in0=kb[r, j][:].rearrange("p t o -> p o t"), in1=b3_of(r, j), op=ADD)
+        def side_add(r):
+            gs[r] = grp.tile([P, P, 4], BF16, name="gs", tag="gs", bufs=1, align_bytes=64)
+            nc.gpsimd.tensor_tensor(out=gs[r][:], in0=kf[r][:], in1=b3_of(r, SIDE), op=ADD)
 
-        def side_exit(r, j):
-            kf[r] = grp.tile([P, P, 4], F32, name="kf", tag="kf", bufs=2)
-            nc.scalar.copy(out=kf[r][:], in_=kb[r, j][:].rearrange("p t o -> p o t"))
+        def quant_k(r, part):
+            if r not in kc:
+                kc[r] = cod.tile([P, 512], U32, name="kc", tag="kc", align_bytes=64)
+                ks[r] = cod.tile([P, 512], U8, name="ks", tag="ks", align_bytes=64)
+            if part == "a":
+                quant(kc[r][:, 0:256], ks[r][:, 0:256], gk[r][:, 0:2, :, :].rearrange("p j o t -> p (j o t)"))
+            elif part == "b":
+                quant(kc[r][:, 256:384], ks[r][:, 256:384], gk[r][:, 2, :, :].rearrange("p o t -> p (o t)"))
+            else:
+                quant(kc[r][:, 384:512], ks[r][:, 384:512], gs[r][:].rearrange("p o t -> p (o t)"))
 
-        def side_add(r, j):
-            nc.gpsimd.tensor_tensor(out=gk[r][:, j, :, :], in0=kf[r][:], in1=b3_of(r, j), op=ADD)
-
-        def quant_k(r):
-            kc[r] = cod.tile([P, 512], U32, name="kc", tag="kc", align_bytes=64)
-            ks[r] = cod.tile([P, 512], U8, name="ks", tag="ks", align_bytes=64)
-            nc.vector.quantize_mx(out=kc[r][:].bitcast(FP8X4), scales=ks[r][:], in_=gk[r][:].rearrange("p j o t -> p (j o t)"))
-
-        def stage2(r):
-            for j in range(4):
-                cols = slice(P * j, P * (j + 1))
+        def stage2(r, blocks):
+            for q in blocks:
+                cols = slice(P * q, P * (q + 1))
                 nc.tensor.matmul_mx(
                     out=acc[:],
                     lhsT=xc[r][:, cols].bitcast(FP8X4),
                     lhsT_scale=xs[r][:, cols],
                     rhs=kc[r][:, cols].bitcast(FP8X4),
                     rhs_scale=ks[r][:, cols],
-                    start=(r == 0 and j == 0),
-                    stop=(r == ROUNDS - 1 and j == 3),
+                    start=(r == 0 and q == blocks[0]),
+                    stop=(r == ROUNDS - 1 and q == 2),
                 )
 
-        def stage1_round(r, j):
-            stage1(r, j)
-            if GP and j == 3:
-                side_exit(r, j)
-
         spread_b3(0, "v")
+        spread_b3(1, "s")
         flip_h(0, 0, "s")
         flip_h(0, 1, "v")
         quant_h(0)
@@ -188,47 +191,55 @@ def tile_ckconv_pa_kernel(tc, x, h_sine, w3, b3, bias, out):
         quant_w(0)
         flip_h(1, 0, "s")
         flip_h(1, 1, "v")
-        quant_h(1)
         flip_w(1)
-        for j in ORDER:
-            stage1_round(0, j)
-        new_gk(0)
-        if GP:
-            side_add(0, 3)
-        flip_w(2)
+        stage1(0, 0)
+        stage1(0, 1)
+        quant_h(1)
         flip_x(0)
+        stage1(0, SIDE)
+        stage1(0, 2)
+        side_add(0)
+        flip_w(2)
+        flip_x(1)
 
         for s in range(ROUNDS):
             nxt = s + 1 < ROUNDS
+            last = s == ROUNDS - 1
             if s == 0:
-                for j in ORDER:
-                    if not (GP and j == 3):
-                        add_b3(s, j)
+                for q in MAIN:
+                    add_b3(s, q)
                 quant_w(1)
-                for j in ORDER:
-                    stage1_round(1, j)
+                for q in [SIDE] + MAIN:
+                    stage1(1, q)
             else:
-                for j in ORDER:
-                    if not (GP and j == 3):
-                        add_b3(s, j)
+                if nxt:
+                    stage1(s + 1, SIDE)
+                if s % 2 == 1 and (s + 1) // 2 + 1 < CIN // 4:
+                    spread_b3((s + 1) // 2 + 1, "s")
+                for q in MAIN:
+                    add_b3(s, q)
                     if nxt:
-                        stage1_round(s + 1, j)
-                stage2(s - 1)
+                        stage1(s + 1, q)
+                stage2(s - 1, [0, 1, 2, 3])
+            if last:
+                quant_k(s, "s")
+                quant_k(s, "a")
+                quant_k(s, "b")
+                stage2(s, [3, 0, 1, 2])
+                break
             quant_x(s)
+            if s == ROUNDS - 2:
+                quant_x(s + 1)
             if s + 2 < ROUNDS:
                 quant_w(s + 2)
-            quant_k(s)
-            if nxt:
-                new_gk(s + 1)
-                if GP:
-                    side_add(s + 1, 3)
+            quant_k(s, "a")
+            quant_k(s, "b")
+            quant_k(s, "s")
+            side_add(s + 1)
             if s + 3 < ROUNDS:
                 flip_w(s + 3)
-            if nxt:
-                flip_x(s + 1)
-            if s % 2 == 0 and s // 2 + 1 < CIN // 4:
-                spread_b3(s // 2 + 1, "s")
-        stage2(ROUNDS - 1)
+            if s + 2 < ROUNDS:
+                flip_x(s + 2)
 
         res = const.tile([P, P], F32, name="res")
         nc.vector.tensor_tensor(out=res[:], in0=acc[:], in1=bias_bc[:], op=ADD)

@@ -36,7 +36,7 @@ def tile_ckconv_pa_kernel(tc, x, h_sine, w3, b3, bias, out):
         hs_view = h_sine.rearrange("(g u p e) h -> g p u (e h)", g=2, u=2, p=P, e=2)
         w_view = w3.rearrange("(o i) h -> o (i h)", i=CIN)
         x_view = x.rearrange("b i l -> b (i l)")
-        hs_sb = [const.tile([P, 2, 1024], BF16, name="hs_sb%d" % g) for g in range(2)]
+        hs_sb = [const.tile([P, 1024], BF16, name="hs_sb%d" % k) for k in range(4)]
         w_sb = [loads.tile([P, 1024], BF16, name="w_sb%d" % r) for r in range(ROUNDS)]
         x_sb = [loads.tile([P, 2048], BF16, name="x_sb%d" % r) for r in range(ROUNDS)]
 
@@ -46,9 +46,13 @@ def tile_ckconv_pa_kernel(tc, x, h_sine, w3, b3, bias, out):
         def load_x(r):
             nc.sync.dma_start(out=x_sb[r][:], in_=x_view[:, 2048 * r : 2048 * (r + 1)])
 
-        nc.sync.dma_start(out=hs_sb[0][:], in_=hs_view[0])
+        def load_h(g):
+            for u in range(2):
+                nc.sync.dma_start(out=hs_sb[2 * g + u][:], in_=hs_view[g][:, u, :])
+
+        load_h(0)
         load_w(0)
-        nc.sync.dma_start(out=hs_sb[1][:], in_=hs_view[1])
+        load_h(1)
         load_w(1)
         for r in range(ROUNDS):
             load_x(r)
@@ -73,12 +77,21 @@ def tile_ckconv_pa_kernel(tc, x, h_sine, w3, b3, bias, out):
             else:
                 nc.scalar.copy(out=dest, in_=src)
 
-        def flip(units, dest, engine):
+        waiting = {"copies": []}
+
+        def flush():
+            for engine, dest, src in waiting["copies"]:
+                leave(engine, dest, src)
+            waiting["copies"] = []
+
+        def flip(units, dest, engine, later=False):
             bank = tps.tile([P, 2, 2, P], F32, name="tbank", tag="tbank")
             for n, (src, col) in enumerate(units):
                 for u in range(2):
                     nc.tensor.transpose(bank[:, n, u, :], src[:, col + P * u : col + P * (u + 1)], ident_f[:])
-            leave(engine, dest.rearrange("p (n r u) -> p n r u", n=2, u=2), bank[:].rearrange("p n u r -> p n r u"))
+            waiting["copies"].append((engine, dest.rearrange("p (n r u) -> p n r u", n=2, u=2), bank[:].rearrange("p n u r -> p n r u")))
+            if not later:
+                flush()
 
         def spread_b3(jb, engine):
             bank = tps.tile([P, 4, P], F32, name="bbank", tag="tbank")
@@ -92,8 +105,8 @@ def tile_ckconv_pa_kernel(tc, x, h_sine, w3, b3, bias, out):
         def flip_h(g, half, engine):
             if half == 0:
                 gh[g] = grp.tile([P, 2048], BF16, name="gh", tag="gh", bufs=2, align_bytes=64)
-            src = hs_sb[g][:].rearrange("p u c -> p (u c)").bitcast(F32)
-            flip([(src, 256 * (2 * half)), (src, 256 * (2 * half + 1))], gh[g][:].bitcast(F32)[:, 512 * half : 512 * (half + 1)], engine)
+            src = hs_sb[2 * g + half][:].bitcast(F32)
+            flip([(src, 0), (src, 256)], gh[g][:].bitcast(F32)[:, 512 * half : 512 * (half + 1)], engine)
 
         def quant(codes, scales, src):
             nc.vector.quantize_mx(out=codes.bitcast(FP8X4), scales=scales, in_=src)
@@ -115,11 +128,15 @@ def tile_ckconv_pa_kernel(tc, x, h_sine, w3, b3, bias, out):
 
         gx, xc, xs = {}, {}, {}
 
-        def flip_x(r):
-            gx[r] = grp.tile([P, 2048], BF16, name="gx", tag="gx", align_bytes=64)
+        def flip_x_half(r, g, later=False):
+            if g == 0:
+                gx[r] = grp.tile([P, 2048], BF16, name="gx", tag="gx", align_bytes=64)
             src = x_sb[r][:].bitcast(F32)
-            for g in range(2):
-                flip([(src, 256 * g), (src, 512 + 256 * g)], gx[r][:].bitcast(F32)[:, 512 * g : 512 * (g + 1)], "s")
+            flip([(src, 256 * g), (src, 512 + 256 * g)], gx[r][:].bitcast(F32)[:, 512 * g : 512 * (g + 1)], "s", later)
+
+        def flip_x(r):
+            flip_x_half(r, 0)
+            flip_x_half(r, 1, True)
 
         def quant_x(r):
             xc[r] = cod.tile([P, 512], U32, name="xc", tag="xc", bufs=4, align_bytes=64)
@@ -145,6 +162,7 @@ def tile_ckconv_pa_kernel(tc, x, h_sine, w3, b3, bias, out):
             if q == SIDE:
                 kf[r] = grp.tile([P, P, 4], F32, name="kf", tag="kf", bufs=2)
                 nc.scalar.copy(out=kf[r][:], in_=kb[r, q][:].rearrange("p t o -> p o t"))
+                flush()
 
         def b3_of(r, q):
             return b3bc[:, 2 * r + q % 2, :].unsqueeze(2).to_broadcast([P, P, 4])
@@ -195,12 +213,13 @@ def tile_ckconv_pa_kernel(tc, x, h_sine, w3, b3, bias, out):
         stage1(0, 0)
         stage1(0, 1)
         quant_h(1)
-        flip_x(0)
-        stage1(0, SIDE)
+        flip_x_half(0, 0)
         stage1(0, 2)
+        stage1(0, SIDE)
         side_add(0)
+        flip_x_half(0, 1)
         flip_w(2)
-        flip_x(1)
+        flip_x_half(1, 0)
 
         for s in range(ROUNDS):
             nxt = s + 1 < ROUNDS
@@ -211,6 +230,7 @@ def tile_ckconv_pa_kernel(tc, x, h_sine, w3, b3, bias, out):
                 quant_w(1)
                 for q in [SIDE] + MAIN:
                     stage1(1, q)
+                flip_x_half(1, 1)
             else:
                 if nxt:
                     stage1(s + 1, SIDE)
@@ -227,14 +247,19 @@ def tile_ckconv_pa_kernel(tc, x, h_sine, w3, b3, bias, out):
                 quant_k(s, "b")
                 stage2(s, [3, 0, 1, 2])
                 break
+            if s == 0:
+                quant_k(s, "b")
+                quant_k(s, "a")
             quant_x(s)
             if s == ROUNDS - 2:
                 quant_x(s + 1)
             if s + 2 < ROUNDS:
                 quant_w(s + 2)
-            quant_k(s, "a")
-            quant_k(s, "b")
+            if s > 0:
+                quant_k(s, "b")
             quant_k(s, "s")
+            if s > 0:
+                quant_k(s, "a")
             side_add(s + 1)
             if s + 3 < ROUNDS:
                 flip_w(s + 3)

@@ -15,8 +15,17 @@ CIN = 32
 ROUNDS = 16
 FLOPS = 2 * 1024 * 4096 * 512 + 2 * 128 * 128 * 32768
 
-SIDE = 3
-MAIN = [0, 1, 2]
+
+def side_of(r):
+    return 1 if r == 0 else 3
+
+
+def main_of(r):
+    return [0, 2, 3] if r == 0 else [0, 1, 2]
+
+
+def place(r, q):
+    return 3 if q == side_of(r) else main_of(r).index(q)
 
 
 def tile_ckconv_pa_kernel(tc, x, h_sine, w3, b3, bias, out):
@@ -136,7 +145,7 @@ def tile_ckconv_pa_kernel(tc, x, h_sine, w3, b3, bias, out):
 
         def flip_x(r):
             flip_x_half(r, 0)
-            flip_x_half(r, 1, True)
+            flip_x_half(r, 1, r < ROUNDS - 1)
 
         def quant_x(r):
             xc[r] = cod.tile([P, 512], U32, name="xc", tag="xc", bufs=4, align_bytes=64)
@@ -159,7 +168,7 @@ def tile_ckconv_pa_kernel(tc, x, h_sine, w3, b3, bias, out):
                     start=True,
                     stop=True,
                 )
-            if q == SIDE:
+            if q == side_of(r):
                 kf[r] = grp.tile([P, P, 4], F32, name="kf", tag="kf", bufs=2)
                 nc.scalar.copy(out=kf[r][:], in_=kb[r, q][:].rearrange("p t o -> p o t"))
                 flush()
@@ -170,11 +179,11 @@ def tile_ckconv_pa_kernel(tc, x, h_sine, w3, b3, bias, out):
         def add_b3(r, q):
             if q == 0:
                 gk[r] = grp.tile([P, 3, P, 4], BF16, name="gk", tag="gk", bufs=2, align_bytes=64)
-            nc.vector.tensor_tensor(out=gk[r][:, q, :, :], in0=kb[r, q][:].rearrange("p t o -> p o t"), in1=b3_of(r, q), op=ADD)
+            nc.vector.tensor_tensor(out=gk[r][:, place(r, q), :, :], in0=kb[r, q][:].rearrange("p t o -> p o t"), in1=b3_of(r, q), op=ADD)
 
         def side_add(r):
             gs[r] = grp.tile([P, P, 4], BF16, name="gs", tag="gs", bufs=1, align_bytes=64)
-            nc.gpsimd.tensor_tensor(out=gs[r][:], in0=kf[r][:], in1=b3_of(r, SIDE), op=ADD)
+            nc.gpsimd.tensor_tensor(out=gs[r][:], in0=kf[r][:], in1=b3_of(r, side_of(r)), op=ADD)
 
         def quant_k(r, part):
             if r not in kc:
@@ -187,17 +196,18 @@ def tile_ckconv_pa_kernel(tc, x, h_sine, w3, b3, bias, out):
             else:
                 quant(kc[r][:, 384:512], ks[r][:, 384:512], gs[r][:].rearrange("p o t -> p (o t)"))
 
-        def stage2(r, blocks):
-            for q in blocks:
+        def stage2(r, banks):
+            for q in banks:
                 cols = slice(P * q, P * (q + 1))
+                kcols = slice(P * place(r, q), P * (place(r, q) + 1))
                 nc.tensor.matmul_mx(
                     out=acc[:],
                     lhsT=xc[r][:, cols].bitcast(FP8X4),
                     lhsT_scale=xs[r][:, cols],
-                    rhs=kc[r][:, cols].bitcast(FP8X4),
-                    rhs_scale=ks[r][:, cols],
-                    start=(r == 0 and q == blocks[0]),
-                    stop=(r == ROUNDS - 1 and q == 2),
+                    rhs=kc[r][:, kcols].bitcast(FP8X4),
+                    rhs_scale=ks[r][:, kcols],
+                    start=(r == 0 and q == banks[0]),
+                    stop=(r == ROUNDS - 1 and q == banks[-1]),
                 )
 
         spread_b3(0, "v")
@@ -213,10 +223,11 @@ def tile_ckconv_pa_kernel(tc, x, h_sine, w3, b3, bias, out):
         stage1(0, 0)
         stage1(0, 1)
         quant_h(1)
+        quant_w(1)
+        side_add(0)
         flip_x_half(0, 0)
         stage1(0, 2)
-        stage1(0, SIDE)
-        side_add(0)
+        stage1(0, 3)
         flip_x_half(0, 1)
         flip_w(2)
         flip_x_half(1, 0)
@@ -224,22 +235,15 @@ def tile_ckconv_pa_kernel(tc, x, h_sine, w3, b3, bias, out):
         for s in range(ROUNDS):
             nxt = s + 1 < ROUNDS
             last = s == ROUNDS - 1
-            if s == 0:
-                for q in MAIN:
-                    add_b3(s, q)
-                quant_w(1)
-                for q in [SIDE] + MAIN:
-                    stage1(1, q)
-                flip_x_half(1, 1)
-            else:
+            for k in range(3):
+                add_b3(s, main_of(s)[k])
                 if nxt:
-                    stage1(s + 1, SIDE)
-                if s % 2 == 1 and (s + 1) // 2 + 1 < CIN // 4:
-                    spread_b3((s + 1) // 2 + 1, "s")
-                for q in MAIN:
-                    add_b3(s, q)
-                    if nxt:
-                        stage1(s + 1, q)
+                    stage1(s + 1, main_of(s + 1)[k])
+                    if k == 0:
+                        stage1(s + 1, side_of(s + 1))
+                        if s % 2 == 1 and (s + 1) // 2 + 1 < CIN // 4:
+                            spread_b3((s + 1) // 2 + 1, "s")
+            if s > 0:
                 stage2(s - 1, [0, 1, 2, 3])
             if last:
                 quant_k(s, "s")
@@ -248,15 +252,14 @@ def tile_ckconv_pa_kernel(tc, x, h_sine, w3, b3, bias, out):
                 stage2(s, [3, 0, 1, 2])
                 break
             if s == 0:
-                quant_k(s, "b")
+                flip_x_half(1, 1)
                 quant_k(s, "a")
             quant_x(s)
             if s == ROUNDS - 2:
                 quant_x(s + 1)
             if s + 2 < ROUNDS:
                 quant_w(s + 2)
-            if s > 0:
-                quant_k(s, "b")
+            quant_k(s, "b")
             quant_k(s, "s")
             if s > 0:
                 quant_k(s, "a")

@@ -152,7 +152,7 @@ def tile_ckconv_pa_kernel(tc, x, h_sine, w3, b3, bias, out):
             xs[r] = cod.tile([P, 512], U8, name="xs", tag="xs", bufs=4, align_bytes=64)
             quant(xc[r][:], xs[r][:], gx[r][:])
 
-        kb, gk, gs, kc, ks, kf = {}, {}, {}, {}, {}, {}
+        kb, ga, gb, kc, ks, kf = {}, {}, {}, {}, {}, {}
 
         def stage1(r, q):
             g, n = q // 2, q % 2
@@ -177,24 +177,28 @@ def tile_ckconv_pa_kernel(tc, x, h_sine, w3, b3, bias, out):
             return b3bc[:, 2 * r + q % 2, :].unsqueeze(2).to_broadcast([P, P, 4])
 
         def add_b3(r, q):
-            if q == 0:
-                gk[r] = grp.tile([P, 3, P, 4], BF16, name="gk", tag="gk", bufs=2, align_bytes=64)
-            nc.vector.tensor_tensor(out=gk[r][:, place(r, q), :, :], in0=kb[r, q][:].rearrange("p t o -> p o t"), in1=b3_of(r, q), op=ADD)
+            k = place(r, q)
+            if k == 0:
+                ga[r] = grp.tile([P, 2, P, 4], BF16, name="ga", tag="ga", bufs=2, align_bytes=64)
+            dest = ga[r][:, k, :, :] if k < 2 else gb[r][:, 0, :, :]
+            nc.vector.tensor_tensor(out=dest, in0=kb[r, q][:].rearrange("p t o -> p o t"), in1=b3_of(r, q), op=ADD)
 
         def side_add(r):
-            gs[r] = grp.tile([P, P, 4], BF16, name="gs", tag="gs", bufs=1, align_bytes=64)
-            nc.gpsimd.tensor_tensor(out=gs[r][:], in0=kf[r][:], in1=b3_of(r, side_of(r)), op=ADD)
+            gb[r] = grp.tile([P, 2, P, 4], BF16, name="gb", tag="gb", bufs=1, align_bytes=64)
+            nc.gpsimd.tensor_tensor(out=gb[r][:, 1, :, :], in0=kf[r][:], in1=b3_of(r, side_of(r)), op=ADD)
 
         def quant_k(r, part):
             if r not in kc:
                 kc[r] = cod.tile([P, 512], U32, name="kc", tag="kc", align_bytes=64)
                 ks[r] = cod.tile([P, 512], U8, name="ks", tag="ks", align_bytes=64)
             if part == "a":
-                quant(kc[r][:, 0:256], ks[r][:, 0:256], gk[r][:, 0:2, :, :].rearrange("p j o t -> p (j o t)"))
+                quant(kc[r][:, 0:256], ks[r][:, 0:256], ga[r][:].rearrange("p j o t -> p (j o t)"))
+            elif part == "bs":
+                quant(kc[r][:, 256:512], ks[r][:, 256:512], gb[r][:].rearrange("p j o t -> p (j o t)"))
             elif part == "b":
-                quant(kc[r][:, 256:384], ks[r][:, 256:384], gk[r][:, 2, :, :].rearrange("p o t -> p (o t)"))
+                quant(kc[r][:, 256:384], ks[r][:, 256:384], gb[r][:, 0, :, :].rearrange("p o t -> p (o t)"))
             else:
-                quant(kc[r][:, 384:512], ks[r][:, 384:512], gs[r][:].rearrange("p o t -> p (o t)"))
+                quant(kc[r][:, 384:512], ks[r][:, 384:512], gb[r][:, 1, :, :].rearrange("p o t -> p (o t)"))
 
         def stage2(r, banks):
             for q in banks:
@@ -211,7 +215,7 @@ def tile_ckconv_pa_kernel(tc, x, h_sine, w3, b3, bias, out):
                 )
 
         spread_b3(0, "v")
-        spread_b3(1, "s")
+        spread_b3(1, "v")
         flip_h(0, 0, "s")
         flip_h(0, 1, "v")
         quant_h(0)
@@ -259,8 +263,7 @@ def tile_ckconv_pa_kernel(tc, x, h_sine, w3, b3, bias, out):
                 quant_x(s + 1)
             if s + 2 < ROUNDS:
                 quant_w(s + 2)
-            quant_k(s, "b")
-            quant_k(s, "s")
+            quant_k(s, "bs")
             if s > 0:
                 quant_k(s, "a")
             side_add(s + 1)

@@ -9,6 +9,7 @@ U32 = mybir.dt.uint32
 U8 = mybir.dt.uint8
 FP8X4 = mybir.dt.float8_e4m3fn_x4
 ADD = mybir.AluOpType.add
+IDENTITY = mybir.ActivationFunctionType.Identity
 
 P = 128
 CIN = 32
@@ -20,12 +21,16 @@ def side_of(r):
     return 1 if r == 0 else 3
 
 
+def turned_of(r):
+    return [2] if r % 2 == 1 else []
+
+
 def main_of(r):
-    return [0, 2, 3] if r == 0 else [0, 1, 2]
+    return [0, 2, 3] if r == 0 else [q for q in [0, 1, 2] if q not in turned_of(r)]
 
 
 def place(r, q):
-    return 3 if q == side_of(r) else main_of(r).index(q)
+    return 3 if q == side_of(r) else (main_of(r) + turned_of(r)).index(q)
 
 
 def tile_ckconv_pa_kernel(tc, x, h_sine, w3, b3, bias, out):
@@ -94,20 +99,20 @@ def tile_ckconv_pa_kernel(tc, x, h_sine, w3, b3, bias, out):
             waiting["copies"] = []
 
         def flip(units, dest, engine, later=False):
-            bank = tps.tile([P, 2, 2, P], F32, name="tbank", tag="tbank")
+            bank = tps.tile([P, len(units), 2, P], F32, name="tbank", tag="tbank")
             for n, (src, col) in enumerate(units):
                 for u in range(2):
                     nc.tensor.transpose(bank[:, n, u, :], src[:, col + P * u : col + P * (u + 1)], ident_f[:])
-            waiting["copies"].append((engine, dest.rearrange("p (n r u) -> p n r u", n=2, u=2), bank[:].rearrange("p n u r -> p n r u")))
+            waiting["copies"].append((engine, dest.rearrange("p (n r u) -> p n r u", r=P, u=2), bank[:].rearrange("p n u r -> p n r u")))
             if not later:
                 flush()
 
         def spread_b3(jb, engine):
-            bank = tps.tile([P, 4, P], F32, name="bbank", tag="tbank")
-            for q in range(4):
-                c = 4 * jb + q
+            bank = tps.tile([P, 8, P], BF16, name="bbank", tag="tbank")
+            for q in range(8):
+                c = 8 * jb + q
                 nc.tensor.matmul(out=bank[:, q, :], lhsT=b3T[:, c : c + 1].to_broadcast([P, P]), rhs=ident_b[:], start=True, stop=True)
-            leave(engine, b3bc[:, 4 * jb : 4 * jb + 4, :], bank[:])
+            leave(engine, b3bc[:, 8 * jb : 8 * (jb + 1), :], bank[:])
 
         gh = {}
 
@@ -173,6 +178,29 @@ def tile_ckconv_pa_kernel(tc, x, h_sine, w3, b3, bias, out):
                 nc.scalar.copy(out=kf[r][:], in_=kb[r, q][:].rearrange("p t o -> p o t"))
                 flush()
 
+        kt = {}
+
+        def stage1_turned(r, q):
+            bank = kps.tile([P, 2, 2, P], F32, name="kbank", tag="kbank")
+            n, c = q % 2, 512 * (q // 2)
+            nc.tensor.matmul_mx(
+                out=bank[:].rearrange("o u e p -> o (u e p)"),
+                lhsT=wc[r][:, P * n : P * (n + 1)].bitcast(FP8X4),
+                lhsT_scale=ws[r][:, P * n : P * (n + 1)],
+                rhs=hs_codes[:, c : c + 512].bitcast(FP8X4),
+                rhs_scale=hs_scales[:, c : c + 512],
+                start=True,
+                stop=True,
+            )
+            kt[r] = grp.tile([P, 2, P, 2], BF16, name="kt", tag="kt", bufs=2)
+            i = 2 * r + n
+            nc.scalar.activation(out=kt[r][:], in_=bank[:].rearrange("o u e p -> o u p e"), func=IDENTITY, bias=b3T[:, i : i + 1], scale=1.0)
+
+        def flip_k(r):
+            src = kt[r][:].rearrange("o u p e -> o (u p e)").bitcast(F32)
+            dest = gb[r][:, 0, :, :].rearrange("p o t -> p (o t)").bitcast(F32)
+            flip([(src, 0)], dest, "s")
+
         def b3_of(r, q):
             return b3bc[:, 2 * r + q % 2, :].unsqueeze(2).to_broadcast([P, P, 4])
 
@@ -215,7 +243,6 @@ def tile_ckconv_pa_kernel(tc, x, h_sine, w3, b3, bias, out):
                 )
 
         spread_b3(0, "v")
-        spread_b3(1, "v")
         flip_h(0, 0, "s")
         flip_h(0, 1, "v")
         quant_h(0)
@@ -239,14 +266,18 @@ def tile_ckconv_pa_kernel(tc, x, h_sine, w3, b3, bias, out):
         for s in range(ROUNDS):
             nxt = s + 1 < ROUNDS
             last = s == ROUNDS - 1
-            for k in range(3):
-                add_b3(s, main_of(s)[k])
-                if nxt:
-                    stage1(s + 1, main_of(s + 1)[k])
-                    if k == 0:
-                        stage1(s + 1, side_of(s + 1))
-                        if s % 2 == 1 and (s + 1) // 2 + 1 < CIN // 4:
-                            spread_b3((s + 1) // 2 + 1, "s")
+            for q in main_of(s):
+                add_b3(s, q)
+            if nxt:
+                main = main_of(s + 1)
+                stage1(s + 1, side_of(s + 1))
+                stage1(s + 1, main[0])
+                for q in turned_of(s + 1):
+                    stage1_turned(s + 1, q)
+                if s % 4 == 1 and s // 4 + 1 < CIN // 8:
+                    spread_b3(s // 4 + 1, "s")
+                for q in main[1:]:
+                    stage1(s + 1, q)
             if s > 0:
                 stage2(s - 1, [0, 1, 2, 3])
             if last:
@@ -263,14 +294,15 @@ def tile_ckconv_pa_kernel(tc, x, h_sine, w3, b3, bias, out):
                 quant_x(s + 1)
             if s + 2 < ROUNDS:
                 quant_w(s + 2)
-            quant_k(s, "bs")
-            if s > 0:
-                quant_k(s, "a")
+            for part in ["bs"] if s == 0 else ["a", "bs"] if turned_of(s) else ["bs", "a"]:
+                quant_k(s, part)
             side_add(s + 1)
             if s + 3 < ROUNDS:
                 flip_w(s + 3)
             if s + 2 < ROUNDS:
                 flip_x(s + 2)
+            if turned_of(s + 1):
+                flip_k(s + 1)
 
         res = const.tile([P, P], F32, name="res")
         nc.vector.tensor_tensor(out=res[:], in0=acc[:], in1=bias_bc[:], op=ADD)

@@ -21,6 +21,16 @@ def side_of(r):
     return 1 if r == 0 else 3
 
 
+def x_turned(s):
+    if s < 0 or s == ROUNDS - 1:
+        return []
+    return [s] if s < ROUNDS - 3 else [s, s + 1] if s == ROUNDS - 3 else [s + 1]
+
+
+def products(s):
+    return [s - 3] if 3 <= s < ROUNDS - 1 else [s - 3, s - 2, s - 1] if s == ROUNDS - 1 else []
+
+
 def turned_of(r):
     return [2] if r % 2 == 1 else []
 
@@ -41,8 +51,8 @@ def tile_ckconv_pa_kernel(tc, x, h_sine, w3, b3, bias, out):
         loads = ctx.enter_context(tc.tile_pool(name="loads", bufs=1))
         grp = ctx.enter_context(tc.tile_pool(name="grp", bufs=3))
         cod = ctx.enter_context(tc.tile_pool(name="cod", bufs=3))
-        tps = ctx.enter_context(tc.psum_pool(name="ps_t", bufs=3))
-        kps = ctx.enter_context(tc.psum_pool(name="ps_k", bufs=4))
+        tps = ctx.enter_context(tc.psum_pool(name="ps_t", bufs=4))
+        kps = ctx.enter_context(tc.psum_pool(name="ps_k", bufs=3))
         aps = ctx.enter_context(tc.psum_pool(name="ps_a", bufs=1))
 
         b3T = const.tile([P, CIN], BF16, name="b3T")
@@ -68,10 +78,11 @@ def tile_ckconv_pa_kernel(tc, x, h_sine, w3, b3, bias, out):
         load_w(0)
         load_h(1)
         load_w(1)
+        load_w(2)
         for r in range(ROUNDS):
+            if r + 3 < ROUNDS:
+                load_w(r + 3)
             load_x(r)
-            if r + 2 < ROUNDS:
-                load_w(r + 2)
         bias_bc = const.tile([P, P], BF16, name="bias_bc")
         nc.sync.dma_start(out=bias_bc[:], in_=bias.partition_broadcast(P))
 
@@ -125,8 +136,9 @@ def tile_ckconv_pa_kernel(tc, x, h_sine, w3, b3, bias, out):
         def quant(codes, scales, src):
             nc.vector.quantize_mx(out=codes.bitcast(FP8X4), scales=scales, in_=src)
 
-        def quant_h(g):
-            quant(hs_codes[:, 512 * g : 512 * (g + 1)], hs_scales[:, 512 * g : 512 * (g + 1)], gh[g][:])
+        def quant_h(g, half):
+            c = 512 * g + 256 * half
+            quant(hs_codes[:, c : c + 256], hs_scales[:, c : c + 256], gh[g][:, 1024 * half : 1024 * (half + 1)])
 
         gw, wc, ws = {}, {}, {}
 
@@ -144,24 +156,25 @@ def tile_ckconv_pa_kernel(tc, x, h_sine, w3, b3, bias, out):
 
         def flip_x_half(r, g, later=False):
             if g == 0:
-                gx[r] = grp.tile([P, 2048], BF16, name="gx", tag="gx", align_bytes=64)
+                gx[r] = grp.tile([P, 2048], BF16, name="gx", tag="gx", bufs=4, align_bytes=64)
             src = x_sb[r][:].bitcast(F32)
             flip([(src, 256 * g), (src, 512 + 256 * g)], gx[r][:].bitcast(F32)[:, 512 * g : 512 * (g + 1)], "s", later)
 
         def flip_x(r):
             flip_x_half(r, 0)
-            flip_x_half(r, 1, r < ROUNDS - 1)
+            flip_x_half(r, 1)
 
         def quant_x(r):
-            xc[r] = cod.tile([P, 512], U32, name="xc", tag="xc", bufs=4, align_bytes=64)
-            xs[r] = cod.tile([P, 512], U8, name="xs", tag="xs", bufs=4, align_bytes=64)
+            xc[r] = cod.tile([P, 512], U32, name="xc", tag="xc", bufs=5, align_bytes=64)
+            xs[r] = cod.tile([P, 512], U8, name="xs", tag="xs", bufs=5, align_bytes=64)
             quant(xc[r][:], xs[r][:], gx[r][:])
 
         kb, ga, gb, kc, ks, kf = {}, {}, {}, {}, {}, {}
 
         def stage1(r, q):
             g, n = q // 2, q % 2
-            kb[r, q] = kps.tile([P, 4, P], F32, name="kbank", tag="kbank")
+            pool, tag = (tps, "tbank") if q == side_of(r) else (kps, "kbank")
+            kb[r, q] = pool.tile([P, 4, P], F32, name="kbank", tag=tag)
             for t in range(4):
                 c = P * (4 * g + t)
                 nc.tensor.matmul_mx(
@@ -181,7 +194,7 @@ def tile_ckconv_pa_kernel(tc, x, h_sine, w3, b3, bias, out):
         kt = {}
 
         def stage1_turned(r, q):
-            bank = kps.tile([P, 2, 2, P], F32, name="kbank", tag="kbank")
+            bank = tps.tile([P, 2, 2, P], F32, name="tbank", tag="tbank")
             n, c = q % 2, 512 * (q // 2)
             nc.tensor.matmul_mx(
                 out=bank[:].rearrange("o u e p -> o (u e p)"),
@@ -217,8 +230,8 @@ def tile_ckconv_pa_kernel(tc, x, h_sine, w3, b3, bias, out):
 
         def quant_k(r, part):
             if r not in kc:
-                kc[r] = cod.tile([P, 512], U32, name="kc", tag="kc", align_bytes=64)
-                ks[r] = cod.tile([P, 512], U8, name="ks", tag="ks", align_bytes=64)
+                kc[r] = cod.tile([P, 512], U32, name="kc", tag="kc", bufs=5, align_bytes=64)
+                ks[r] = cod.tile([P, 512], U8, name="ks", tag="ks", bufs=5, align_bytes=64)
             if part == "a":
                 quant(kc[r][:, 0:256], ks[r][:, 0:256], ga[r][:].rearrange("p j o t -> p (j o t)"))
             elif part == "bs":
@@ -245,64 +258,68 @@ def tile_ckconv_pa_kernel(tc, x, h_sine, w3, b3, bias, out):
         spread_b3(0, "v")
         flip_h(0, 0, "s")
         flip_h(0, 1, "v")
-        quant_h(0)
+        quant_h(0, 0)
+        quant_h(0, 1)
         flip_w(0)
+        spread_b3(1, "s")
         quant_w(0)
         flip_h(1, 0, "s")
         flip_h(1, 1, "v")
         flip_w(1)
         stage1(0, 0)
         stage1(0, 1)
-        quant_h(1)
+        quant_h(1, 0)
+        quant_h(1, 1)
         quant_w(1)
         side_add(0)
-        flip_x_half(0, 0)
         stage1(0, 2)
         stage1(0, 3)
-        flip_x_half(0, 1)
+        for q in turned_of(1):
+            stage1_turned(1, q)
         flip_w(2)
-        flip_x_half(1, 0)
+        spread_b3(2, "s")
 
         for s in range(ROUNDS):
             nxt = s + 1 < ROUNDS
             last = s == ROUNDS - 1
+            if last:
+                for r in x_turned(s - 2):
+                    quant_x(r)
             for q in main_of(s):
                 add_b3(s, q)
             if nxt:
                 main = main_of(s + 1)
-                stage1(s + 1, side_of(s + 1))
                 stage1(s + 1, main[0])
-                for q in turned_of(s + 1):
-                    stage1_turned(s + 1, q)
-                if s % 4 == 1 and s // 4 + 1 < CIN // 8:
+                stage1(s + 1, side_of(s + 1))
+                if s == 9 and s // 4 + 1 < CIN // 8:
                     spread_b3(s // 4 + 1, "s")
                 for q in main[1:]:
                     stage1(s + 1, q)
-            if s > 0:
-                stage2(s - 1, [0, 1, 2, 3])
+            for r in products(s):
+                stage2(r, [0, 1, 2, 3])
             if last:
                 quant_k(s, "s")
                 quant_k(s, "a")
+                for r in x_turned(s - 1):
+                    quant_x(r)
                 quant_k(s, "b")
                 stage2(s, [3, 0, 1, 2])
                 break
-            if s == 0:
-                flip_x_half(1, 1)
-                quant_k(s, "a")
-            quant_x(s)
-            if s == ROUNDS - 2:
-                quant_x(s + 1)
             if s + 2 < ROUNDS:
                 quant_w(s + 2)
-            for part in ["bs"] if s == 0 else ["a", "bs"] if turned_of(s) else ["bs", "a"]:
-                quant_k(s, part)
+            for q in turned_of(s + 2) if s + 2 < ROUNDS else []:
+                stage1_turned(s + 2, q)
+            for r in x_turned(s - 2):
+                quant_x(r)
+            quant_k(s, "bs")
+            quant_k(s, "a")
             side_add(s + 1)
             if s + 3 < ROUNDS:
                 flip_w(s + 3)
-            if s + 2 < ROUNDS:
-                flip_x(s + 2)
             if turned_of(s + 1):
                 flip_k(s + 1)
+            for r in x_turned(s):
+                flip_x(r)
 
         res = const.tile([P, P], F32, name="res")
         nc.vector.tensor_tensor(out=res[:], in0=acc[:], in1=bias_bc[:], op=ADD)

@@ -255,6 +255,11 @@ def tile_ckconv_pa_kernel(tc, x, h_sine, w3, b3, bias, out):
                     stop=(r == ROUNDS - 1 and q == banks[-1]),
                 )
 
+        warm = const.tile([P, 512], BF16, name="warm")
+        nc.vector.memset(warm[:], 0.0)
+        for k in range(4):
+            bank = tps.tile([P, 512], F32, name="wbank", tag="tbank")
+            nc.tensor.matmul(out=bank[:], lhsT=ident_b[:], rhs=warm[:], start=True, stop=True)
         spread_b3(0, "v")
         flip_h(0, 0, "s")
         flip_h(0, 1, "v")
@@ -268,6 +273,7 @@ def tile_ckconv_pa_kernel(tc, x, h_sine, w3, b3, bias, out):
         flip_w(1)
         stage1(0, 0)
         stage1(0, 1)
+        flip_w(2)
         quant_h(1, 0)
         quant_h(1, 1)
         quant_w(1)
@@ -276,7 +282,6 @@ def tile_ckconv_pa_kernel(tc, x, h_sine, w3, b3, bias, out):
         stage1(0, 3)
         for q in turned_of(1):
             stage1_turned(1, q)
-        flip_w(2)
         spread_b3(2, "s")
 
         for s in range(ROUNDS):

@@ -22,9 +22,10 @@ def side_of(r):
 
 
 def x_turned(s):
+    n = ROUNDS - 4
     if s < 0 or s == ROUNDS - 1:
         return []
-    return [s] if s < ROUNDS - 3 else [s, s + 1] if s == ROUNDS - 3 else [s + 1]
+    return [s] if s < n else [n, n + 1] if s == n else [s + 1]
 
 
 def products(s):
@@ -32,7 +33,7 @@ def products(s):
 
 
 def turned_of(r):
-    return [2] if r % 2 == 1 else []
+    return [2] if r % 2 == 1 and r > 1 else []
 
 
 def main_of(r):
@@ -40,7 +41,7 @@ def main_of(r):
 
 
 def place(r, q):
-    return 3 if q == side_of(r) else (main_of(r) + turned_of(r)).index(q)
+    return 3 if q == side_of(r) else (main_of(r)[:1] + turned_of(r) + main_of(r)[1:]).index(q)
 
 
 def tile_ckconv_pa_kernel(tc, x, h_sine, w3, b3, bias, out):
@@ -211,7 +212,8 @@ def tile_ckconv_pa_kernel(tc, x, h_sine, w3, b3, bias, out):
 
         def flip_k(r):
             src = kt[r][:].rearrange("o u p e -> o (u p e)").bitcast(F32)
-            dest = gb[r][:, 0, :, :].rearrange("p o t -> p (o t)").bitcast(F32)
+            ga[r] = grp.tile([P, 2, P, 4], BF16, name="ga", tag="ga", bufs=3, align_bytes=64)
+            dest = ga[r][:, 1, :, :].rearrange("p o t -> p (o t)").bitcast(F32)
             flip([(src, 0)], dest, "s")
 
         def b3_of(r, q):
@@ -219,8 +221,8 @@ def tile_ckconv_pa_kernel(tc, x, h_sine, w3, b3, bias, out):
 
         def add_b3(r, q):
             k = place(r, q)
-            if k == 0:
-                ga[r] = grp.tile([P, 2, P, 4], BF16, name="ga", tag="ga", bufs=2, align_bytes=64)
+            if r not in ga:
+                ga[r] = grp.tile([P, 2, P, 4], BF16, name="ga", tag="ga", bufs=3, align_bytes=64)
             dest = ga[r][:, k, :, :] if k < 2 else gb[r][:, 0, :, :]
             nc.vector.tensor_tensor(out=dest, in0=kb[r, q][:].rearrange("p t o -> p o t"), in1=b3_of(r, q), op=ADD)
 
@@ -255,11 +257,6 @@ def tile_ckconv_pa_kernel(tc, x, h_sine, w3, b3, bias, out):
                     stop=(r == ROUNDS - 1 and q == banks[-1]),
                 )
 
-        warm = const.tile([P, 512], BF16, name="warm")
-        nc.vector.memset(warm[:], 0.0)
-        for k in range(4):
-            bank = tps.tile([P, 512], F32, name="wbank", tag="tbank")
-            nc.tensor.matmul(out=bank[:], lhsT=ident_b[:], rhs=warm[:], start=True, stop=True)
         spread_b3(0, "v")
         flip_h(0, 0, "s")
         flip_h(0, 1, "v")
@@ -303,12 +300,11 @@ def tile_ckconv_pa_kernel(tc, x, h_sine, w3, b3, bias, out):
             for r in products(s):
                 stage2(r, [0, 1, 2, 3])
             if last:
-                quant_k(s, "s")
                 quant_k(s, "a")
                 for r in x_turned(s - 1):
                     quant_x(r)
-                quant_k(s, "b")
-                stage2(s, [3, 0, 1, 2])
+                quant_k(s, "bs")
+                stage2(s, [0, 2, 1, 3])
                 break
             if s + 2 < ROUNDS:
                 quant_w(s + 2)
@@ -319,10 +315,10 @@ def tile_ckconv_pa_kernel(tc, x, h_sine, w3, b3, bias, out):
             quant_k(s, "bs")
             quant_k(s, "a")
             side_add(s + 1)
-            if s + 3 < ROUNDS:
-                flip_w(s + 3)
             if turned_of(s + 1):
                 flip_k(s + 1)
+            if s + 3 < ROUNDS:
+                flip_w(s + 3)
             for r in x_turned(s):
                 flip_x(r)
 

@@ -93,8 +93,8 @@ def tile_ckconv_pa_kernel(tc, x, h_sine, w3, b3, bias, out):
         make_identity(nc, ident_f[:])
 
         b3bc = const.tile([P, CIN, P], BF16, name="b3bc")
-        hs_codes = const.tile([P, 1024], U32, name="hs_codes", align_bytes=64)
-        hs_scales = const.tile([P, 1024], U8, name="hs_scales", align_bytes=64)
+        hs_codes = const.tile([P, 1024], U32, name="hs_codes", align_bytes=256)
+        hs_scales = const.tile([P, 1024], U8, name="hs_scales", align_bytes=256)
         acc = aps.tile([P, P], F32, name="acc")
 
         def leave(engine, dest, src):
@@ -149,8 +149,8 @@ def tile_ckconv_pa_kernel(tc, x, h_sine, w3, b3, bias, out):
             flip([(src, 0), (src, 256)], gw[r][:].bitcast(F32), "s")
 
         def quant_w(r):
-            wc[r] = cod.tile([P, 256], U32, name="wc", tag="wc", align_bytes=64)
-            ws[r] = cod.tile([P, 256], U8, name="ws", tag="ws", align_bytes=64)
+            wc[r] = cod.tile([P, 256], U32, name="wc", tag="wc", align_bytes=256)
+            ws[r] = cod.tile([P, 256], U8, name="ws", tag="ws", align_bytes=256)
             quant(wc[r][:], ws[r][:], gw[r][:])
 
         gx, xc, xs = {}, {}, {}
@@ -166,8 +166,8 @@ def tile_ckconv_pa_kernel(tc, x, h_sine, w3, b3, bias, out):
             flip_x_half(r, 1)
 
         def quant_x(r):
-            xc[r] = cod.tile([P, 512], U32, name="xc", tag="xc", bufs=5, align_bytes=64)
-            xs[r] = cod.tile([P, 512], U8, name="xs", tag="xs", bufs=5, align_bytes=64)
+            xc[r] = cod.tile([P, 512], U32, name="xc", tag="xc", bufs=5, align_bytes=256)
+            xs[r] = cod.tile([P, 512], U8, name="xs", tag="xs", bufs=5, align_bytes=256)
             quant(xc[r][:], xs[r][:], gx[r][:])
 
         kb, ga, gb, kc, ks, kf = {}, {}, {}, {}, {}, {}
@@ -232,8 +232,8 @@ def tile_ckconv_pa_kernel(tc, x, h_sine, w3, b3, bias, out):
 
         def quant_k(r, part):
             if r not in kc:
-                kc[r] = cod.tile([P, 512], U32, name="kc", tag="kc", bufs=5, align_bytes=64)
-                ks[r] = cod.tile([P, 512], U8, name="ks", tag="ks", bufs=5, align_bytes=64)
+                kc[r] = cod.tile([P, 512], U32, name="kc", tag="kc", bufs=5, align_bytes=256)
+                ks[r] = cod.tile([P, 512], U8, name="ks", tag="ks", bufs=5, align_bytes=256)
             if part == "a":
                 quant(kc[r][:, 0:256], ks[r][:, 0:256], ga[r][:].rearrange("p j o t -> p (j o t)"))
             elif part == "bs":

@@ -22,10 +22,9 @@ def side_of(r):
 
 
 def x_turned(s):
-    n = ROUNDS - 4
     if s < 0 or s == ROUNDS - 1:
         return []
-    return [s] if s < n else [n, n + 1] if s == n else [s + 1]
+    return [s] if s < ROUNDS - 3 else [s, s + 1] if s == ROUNDS - 3 else [s + 1]
 
 
 def products(s):

@@ -32,7 +32,7 @@ def products(s):
 
 
 def turned_of(r):
-    return [2] if r % 2 == 1 and r > 1 else []
+    return [2] if r % 2 == 1 else []
 
 
 def main_of(r):
@@ -55,8 +55,8 @@ def tile_ckconv_pa_kernel(tc, x, h_sine, w3, b3, bias, out):
         kps = ctx.enter_context(tc.psum_pool(name="ps_k", bufs=3))
         aps = ctx.enter_context(tc.psum_pool(name="ps_a", bufs=1))
 
-        b3T = const.tile([P, CIN], BF16, name="b3T")
-        nc.sync.dma_start(out=b3T[:], in_=b3.rearrange("(o i) -> o i", i=CIN))
+        b3T = const.tile([P, 4, CIN], BF16, name="b3T")
+        nc.sync.dma_start(out=b3T[:], in_=b3.rearrange("(o i) -> o i", i=CIN).unsqueeze(1).to_broadcast([P, 4, CIN]))
         hs_view = h_sine.rearrange("(g u p e) h -> g p u (e h)", g=2, u=2, p=P, e=2)
         w_view = w3.rearrange("(o i) h -> o (i h)", i=CIN)
         x_view = x.rearrange("b i l -> b (i l)")
@@ -74,24 +74,42 @@ def tile_ckconv_pa_kernel(tc, x, h_sine, w3, b3, bias, out):
             for u in range(2):
                 nc.sync.dma_start(out=hs_sb[2 * g + u][:], in_=hs_view[g][:, u, :])
 
-        load_h(0)
-        load_w(0)
-        load_h(1)
-        load_w(1)
-        load_w(2)
-        for r in range(ROUNDS):
-            if r + 3 < ROUNDS:
-                load_w(r + 3)
-            load_x(r)
-        bias_bc = const.tile([P, P], BF16, name="bias_bc")
-        nc.sync.dma_start(out=bias_bc[:], in_=bias.partition_broadcast(P))
 
         ident_f = const.tile([P, P], F32, name="ident_f")
         ident_b = const.tile([P, P], BF16, name="ident_b")
         make_identity(nc, ident_b[:])
         make_identity(nc, ident_f[:])
 
+        load_h(0)
+        load_w(0)
+        load_h(1)
+        load_w(1)
+        load_w(2)
         b3bc = const.tile([P, CIN, P], BF16, name="b3bc")
+        scratch = out.rearrange("b o z -> (b o z)")[0 : CIN * P // 2]
+
+        def park_b3():
+            bank = tps.tile([P, P], BF16, name="rbank", tag="tbank")
+            nc.tensor.transpose(bank[:], b3T[:].rearrange("p k i -> p (k i)"), ident_b[:])
+            rows = const.tile([P, P], BF16, name="b3rows")
+            nc.vector.tensor_copy(out=rows[:], in_=bank[:])
+            nc.sync.dma_start(out=scratch.rearrange("(i w) -> i w", i=CIN), in_=rows[0:CIN, :].bitcast(F32))
+
+        def fetch_b3(lo, hi):
+            nc.sync.dma_start(
+                out=b3bc[:, lo:hi, :].rearrange("p i o -> p (i o)").bitcast(F32),
+                in_=scratch[lo * P // 2 : hi * P // 2].partition_broadcast(P),
+            )
+
+        park_b3()
+        for r in range(ROUNDS):
+            if r + 3 < ROUNDS:
+                load_w(r + 3)
+            load_x(r)
+            if r == 3:
+                fetch_b3(8, CIN)
+        bias_bc = const.tile([P, P], BF16, name="bias_bc")
+        nc.sync.dma_start(out=bias_bc[:], in_=bias.partition_broadcast(P))
         hs_codes = const.tile([P, 1024], U32, name="hs_codes", align_bytes=256)
         hs_scales = const.tile([P, 1024], U8, name="hs_scales", align_bytes=256)
         acc = aps.tile([P, P], F32, name="acc")
@@ -122,7 +140,7 @@ def tile_ckconv_pa_kernel(tc, x, h_sine, w3, b3, bias, out):
             bank = tps.tile([P, 8, P], BF16, name="bbank", tag="tbank")
             for q in range(8):
                 c = 8 * jb + q
-                nc.tensor.matmul(out=bank[:, q, :], lhsT=b3T[:, c : c + 1].to_broadcast([P, P]), rhs=ident_b[:], start=True, stop=True)
+                nc.tensor.matmul(out=bank[:, q, :], lhsT=b3T[:, 0, c : c + 1].to_broadcast([P, P]), rhs=ident_b[:], start=True, stop=True)
             leave(engine, b3bc[:, 8 * jb : 8 * (jb + 1), :], bank[:])
 
         gh = {}
@@ -207,7 +225,7 @@ def tile_ckconv_pa_kernel(tc, x, h_sine, w3, b3, bias, out):
             )
             kt[r] = grp.tile([P, 2, P, 2], BF16, name="kt", tag="kt", bufs=2)
             i = 2 * r + n
-            nc.scalar.activation(out=kt[r][:], in_=bank[:].rearrange("o u e p -> o u p e"), func=IDENTITY, bias=b3T[:, i : i + 1], scale=1.0)
+            nc.scalar.activation(out=kt[r][:], in_=bank[:].rearrange("o u e p -> o u p e"), func=IDENTITY, bias=b3T[:, 0, i : i + 1], scale=1.0)
 
         def flip_k(r):
             src = kt[r][:].rearrange("o u p e -> o (u p e)").bitcast(F32)
@@ -262,7 +280,6 @@ def tile_ckconv_pa_kernel(tc, x, h_sine, w3, b3, bias, out):
         quant_h(0, 0)
         quant_h(0, 1)
         flip_w(0)
-        spread_b3(1, "s")
         quant_w(0)
         flip_h(1, 0, "s")
         flip_h(1, 1, "v")
@@ -278,7 +295,6 @@ def tile_ckconv_pa_kernel(tc, x, h_sine, w3, b3, bias, out):
         stage1(0, 3)
         for q in turned_of(1):
             stage1_turned(1, q)
-        spread_b3(2, "s")
 
         for s in range(ROUNDS):
             nxt = s + 1 < ROUNDS
@@ -292,8 +308,6 @@ def tile_ckconv_pa_kernel(tc, x, h_sine, w3, b3, bias, out):
                 main = main_of(s + 1)
                 stage1(s + 1, main[0])
                 stage1(s + 1, side_of(s + 1))
-                if s == 9 and s // 4 + 1 < CIN // 8:
-                    spread_b3(s // 4 + 1, "s")
                 for q in main[1:]:
                     stage1(s + 1, q)
             for r in products(s):
@@ -314,10 +328,10 @@ def tile_ckconv_pa_kernel(tc, x, h_sine, w3, b3, bias, out):
             quant_k(s, "bs")
             quant_k(s, "a")
             side_add(s + 1)
-            if turned_of(s + 1):
-                flip_k(s + 1)
             if s + 3 < ROUNDS:
                 flip_w(s + 3)
+            if turned_of(s + 1):
+                flip_k(s + 1)
             for r in x_turned(s):
                 flip_x(r)
 

@@ -55,8 +55,8 @@ def tile_ckconv_pa_kernel(tc, x, h_sine, w3, b3, bias, out):
         kps = ctx.enter_context(tc.psum_pool(name="ps_k", bufs=3))
         aps = ctx.enter_context(tc.psum_pool(name="ps_a", bufs=1))
 
-        b3T = const.tile([P, 4, CIN], BF16, name="b3T")
-        nc.sync.dma_start(out=b3T[:], in_=b3.rearrange("(o i) -> o i", i=CIN).unsqueeze(1).to_broadcast([P, 4, CIN]))
+        b3T = const.tile([P, CIN], BF16, name="b3T")
+        nc.sync.dma_start(out=b3T[:], in_=b3.rearrange("(o i) -> o i", i=CIN))
         hs_view = h_sine.rearrange("(g u p e) h -> g p u (e h)", g=2, u=2, p=P, e=2)
         w_view = w3.rearrange("(o i) h -> o (i h)", i=CIN)
         x_view = x.rearrange("b i l -> b (i l)")
@@ -80,36 +80,26 @@ def tile_ckconv_pa_kernel(tc, x, h_sine, w3, b3, bias, out):
         make_identity(nc, ident_b[:])
         make_identity(nc, ident_f[:])
 
+        b3T4 = const.tile([P, 4, CIN], BF16, name="b3T4")
+        b3rows = const.tile([P, P], BF16, name="b3rows")
+        scratch = out.rearrange("b o z -> (b o z)")[0 : CIN * P // 2]
+
+        bias_bc = const.tile([P, P], BF16, name="bias_bc")
         load_h(0)
         load_w(0)
         load_h(1)
         load_w(1)
         load_w(2)
-        b3bc = const.tile([P, CIN, P], BF16, name="b3bc")
-        scratch = out.rearrange("b o z -> (b o z)")[0 : CIN * P // 2]
+        nc.sync.dma_start(out=b3T4[:], in_=b3.rearrange("(o i) -> o i", i=CIN).unsqueeze(1).to_broadcast([P, 4, CIN]))
 
-        def park_b3():
-            bank = tps.tile([P, P], BF16, name="rbank", tag="tbank")
-            nc.tensor.transpose(bank[:], b3T[:].rearrange("p k i -> p (k i)"), ident_b[:])
-            rows = const.tile([P, P], BF16, name="b3rows")
-            nc.vector.tensor_copy(out=rows[:], in_=bank[:])
-            nc.sync.dma_start(out=scratch.rearrange("(i w) -> i w", i=CIN), in_=rows[0:CIN, :].bitcast(F32))
-
-        def fetch_b3(lo, hi):
-            nc.sync.dma_start(
-                out=b3bc[:, lo:hi, :].rearrange("p i o -> p (i o)").bitcast(F32),
-                in_=scratch[lo * P // 2 : hi * P // 2].partition_broadcast(P),
-            )
-
-        park_b3()
-        for r in range(ROUNDS):
+        def load_round(r):
             if r + 3 < ROUNDS:
                 load_w(r + 3)
             load_x(r)
-            if r == 3:
-                fetch_b3(8, CIN)
-        bias_bc = const.tile([P, P], BF16, name="bias_bc")
-        nc.sync.dma_start(out=bias_bc[:], in_=bias.partition_broadcast(P))
+
+        for r in range(5):
+            load_round(r)
+        b3bc = const.tile([P, CIN, P], BF16, name="b3bc")
         hs_codes = const.tile([P, 1024], U32, name="hs_codes", align_bytes=256)
         hs_scales = const.tile([P, 1024], U8, name="hs_scales", align_bytes=256)
         acc = aps.tile([P, P], F32, name="acc")
@@ -140,8 +130,23 @@ def tile_ckconv_pa_kernel(tc, x, h_sine, w3, b3, bias, out):
             bank = tps.tile([P, 8, P], BF16, name="bbank", tag="tbank")
             for q in range(8):
                 c = 8 * jb + q
-                nc.tensor.matmul(out=bank[:, q, :], lhsT=b3T[:, 0, c : c + 1].to_broadcast([P, P]), rhs=ident_b[:], start=True, stop=True)
+                nc.tensor.matmul(out=bank[:, q, :], lhsT=b3T[:, c : c + 1].to_broadcast([P, P]), rhs=ident_b[:], start=True, stop=True)
             leave(engine, b3bc[:, 8 * jb : 8 * (jb + 1), :], bank[:])
+
+        def park_b3():
+            bank = tps.tile([P, P], BF16, name="rbank", tag="tbank")
+            nc.tensor.transpose(bank[:], b3T4[:].rearrange("p k i -> p (k i)"), ident_b[:])
+            nc.scalar.copy(out=b3rows[:], in_=bank[:])
+            nc.sync.dma_start(out=scratch.rearrange("(i w) -> i w", i=CIN), in_=b3rows[0:CIN, :].bitcast(F32))
+            for r in range(5, 7):
+                load_round(r)
+            nc.sync.dma_start(
+                out=b3bc[:, 16:CIN, :].rearrange("p i o -> p (i o)").bitcast(F32),
+                in_=scratch[16 * P // 2 :].partition_broadcast(P),
+            )
+            for r in range(7, ROUNDS):
+                load_round(r)
+            nc.sync.dma_start(out=bias_bc[:], in_=bias.partition_broadcast(P))
 
         gh = {}
 
@@ -225,7 +230,7 @@ def tile_ckconv_pa_kernel(tc, x, h_sine, w3, b3, bias, out):
             )
             kt[r] = grp.tile([P, 2, P, 2], BF16, name="kt", tag="kt", bufs=2)
             i = 2 * r + n
-            nc.scalar.activation(out=kt[r][:], in_=bank[:].rearrange("o u e p -> o u p e"), func=IDENTITY, bias=b3T[:, 0, i : i + 1], scale=1.0)
+            nc.scalar.activation(out=kt[r][:], in_=bank[:].rearrange("o u e p -> o u p e"), func=IDENTITY, bias=b3T[:, i : i + 1], scale=1.0)
 
         def flip_k(r):
             src = kt[r][:].rearrange("o u p e -> o (u p e)").bitcast(F32)
@@ -280,6 +285,7 @@ def tile_ckconv_pa_kernel(tc, x, h_sine, w3, b3, bias, out):
         quant_h(0, 0)
         quant_h(0, 1)
         flip_w(0)
+        spread_b3(1, "s")
         quant_w(0)
         flip_h(1, 0, "s")
         flip_h(1, 1, "v")
@@ -287,6 +293,7 @@ def tile_ckconv_pa_kernel(tc, x, h_sine, w3, b3, bias, out):
         stage1(0, 0)
         stage1(0, 1)
         flip_w(2)
+        park_b3()
         quant_h(1, 0)
         quant_h(1, 1)
         quant_w(1)

@@ -39,6 +39,10 @@ def main_of(r):
     return [0, 2, 3] if r == 0 else [q for q in [0, 1, 2] if q not in turned_of(r)]
 
 
+def has_third(r):
+    return len(main_of(r)) == 3
+
+
 def place(r, q):
     return 3 if q == side_of(r) else (main_of(r)[:1] + turned_of(r) + main_of(r)[1:]).index(q)
 
@@ -241,16 +245,20 @@ def tile_ckconv_pa_kernel(tc, x, h_sine, w3, b3, bias, out):
         def b3_of(r, q):
             return b3bc[:, 2 * r + q % 2, :].unsqueeze(2).to_broadcast([P, P, 4])
 
-        def add_b3(r, q):
+        gt = {}
+
+        def add_b3(r, q, o0=0, o1=P):
             k = place(r, q)
             if r not in ga:
                 ga[r] = grp.tile([P, 2, P, 4], BF16, name="ga", tag="ga", bufs=3, align_bytes=64)
-            dest = ga[r][:, k, :, :] if k < 2 else gb[r][:, 0, :, :]
-            nc.vector.tensor_tensor(out=dest, in0=kb[r, q][:].rearrange("p t o -> p o t"), in1=b3_of(r, q), op=ADD)
+            if k == 2 and r not in gt:
+                gt[r] = grp.tile([P, P, 4], BF16, name="gt", tag="gt", bufs=3, align_bytes=64)
+            dest = ga[r][:, k, o0:o1, :] if k < 2 else gt[r][:, o0:o1, :]
+            nc.vector.tensor_tensor(out=dest, in0=kb[r, q][:, :, o0:o1].rearrange("p t o -> p o t"), in1=b3_of(r, q)[:, o0:o1, :], op=ADD)
 
         def side_add(r):
-            gb[r] = grp.tile([P, 2, P, 4], BF16, name="gb", tag="gb", bufs=1, align_bytes=64)
-            nc.gpsimd.tensor_tensor(out=gb[r][:, 1, :, :], in0=kf[r][:], in1=b3_of(r, side_of(r)), op=ADD)
+            gb[r] = grp.tile([P, P, 4], BF16, name="gb", tag="gb", bufs=1, align_bytes=64)
+            nc.gpsimd.tensor_tensor(out=gb[r][:], in0=kf[r][:], in1=b3_of(r, side_of(r)), op=ADD)
 
         def quant_k(r, part):
             if r not in kc:
@@ -258,12 +266,10 @@ def tile_ckconv_pa_kernel(tc, x, h_sine, w3, b3, bias, out):
                 ks[r] = cod.tile([P, 512], U8, name="ks", tag="ks", bufs=5, align_bytes=256)
             if part == "a":
                 quant(kc[r][:, 0:256], ks[r][:, 0:256], ga[r][:].rearrange("p j o t -> p (j o t)"))
-            elif part == "bs":
-                quant(kc[r][:, 256:512], ks[r][:, 256:512], gb[r][:].rearrange("p j o t -> p (j o t)"))
             elif part == "b":
-                quant(kc[r][:, 256:384], ks[r][:, 256:384], gb[r][:, 0, :, :].rearrange("p o t -> p (o t)"))
+                quant(kc[r][:, 256:384], ks[r][:, 256:384], gt[r][:].rearrange("p o t -> p (o t)"))
             else:
-                quant(kc[r][:, 384:512], ks[r][:, 384:512], gb[r][:, 1, :, :].rearrange("p o t -> p (o t)"))
+                quant(kc[r][:, 384:512], ks[r][:, 384:512], gb[r][:].rearrange("p o t -> p (o t)"))
 
         def stage2(r, banks):
             for q in banks:
@@ -309,8 +315,12 @@ def tile_ckconv_pa_kernel(tc, x, h_sine, w3, b3, bias, out):
             if last:
                 for r in x_turned(s - 2):
                     quant_x(r)
-            for q in main_of(s):
+            if s > 0 and has_third(s - 1):
+                add_b3(s - 1, main_of(s - 1)[2], P // 2, P)
+            for q in main_of(s)[:2]:
                 add_b3(s, q)
+            if has_third(s):
+                add_b3(s, main_of(s)[2], 0, P // 2)
             if nxt:
                 main = main_of(s + 1)
                 stage1(s + 1, main[0])
@@ -318,12 +328,15 @@ def tile_ckconv_pa_kernel(tc, x, h_sine, w3, b3, bias, out):
                 for q in main[1:]:
                     stage1(s + 1, q)
             for r in products(s):
-                stage2(r, [0, 1, 2, 3])
+                stage2(r, [q for q in [0, 1, 2, 3] if not (last and r == s - 1 and q == main_of(r)[2])])
             if last:
                 quant_k(s, "a")
+                quant_k(s - 1, "b")
                 for r in x_turned(s - 1):
                     quant_x(r)
-                quant_k(s, "bs")
+                quant_k(s, "b")
+                quant_k(s, "s")
+                stage2(s - 1, [main_of(s - 1)[2]])
                 stage2(s, [0, 2, 1, 3])
                 break
             if s + 2 < ROUNDS:
@@ -332,7 +345,11 @@ def tile_ckconv_pa_kernel(tc, x, h_sine, w3, b3, bias, out):
                 stage1_turned(s + 2, q)
             for r in x_turned(s - 2):
                 quant_x(r)
-            quant_k(s, "bs")
+            if s > 0 and has_third(s - 1):
+                quant_k(s - 1, "b")
+            if not has_third(s):
+                quant_k(s, "b")
+            quant_k(s, "s")
             quant_k(s, "a")
             side_add(s + 1)
             if s + 3 < ROUNDS:

@@ -79,6 +79,8 @@ def tile_ckconv_pa_kernel(tc, x, h_sine, w3, b3, bias, out):
                 nc.sync.dma_start(out=hs_sb[2 * g + u][:], in_=hs_view[g][:, u, :])
 
 
+        zeros = const.tile([P, P], BF16, name="zeros")
+        nc.gpsimd.memset(zeros[:], 0.0)
         ident_f = const.tile([P, P], F32, name="ident_f")
         ident_b = const.tile([P, P], BF16, name="ident_b")
         make_identity(nc, ident_b[:])
@@ -284,6 +286,9 @@ def tile_ckconv_pa_kernel(tc, x, h_sine, w3, b3, bias, out):
                     start=(r == 0 and q == banks[0]),
                     stop=(r == ROUNDS - 1 and q == banks[-1]),
                 )
+
+        for k in range(12):
+            nc.tensor.matmul(out=acc[:], lhsT=zeros[:], rhs=zeros[:], start=True, stop=True)
 
         spread_b3(0, "v")
         flip_h(0, 0, "s")

@@ -17,6 +17,18 @@ ROUNDS = 16
 FLOPS = 2 * 1024 * 4096 * 512 + 2 * 128 * 128 * 32768
 
 
+def main_of(r):
+    return [0, 2] if r == 0 else [0, 1]
+
+
+def third_of(r):
+    return 3 if r == 0 else 2
+
+
+def turned_of(r):
+    return 2
+
+
 def side_of(r):
     return 1 if r == 0 else 3
 
@@ -29,22 +41,6 @@ def x_turned(s):
 
 def products(s):
     return [s - 3] if 3 <= s < ROUNDS - 1 else [s - 3, s - 2, s - 1] if s == ROUNDS - 1 else []
-
-
-def turned_of(r):
-    return [2] if r % 2 == 1 else []
-
-
-def main_of(r):
-    return [0, 2, 3] if r == 0 else [q for q in [0, 1, 2] if q not in turned_of(r)]
-
-
-def has_third(r):
-    return len(main_of(r)) == 3
-
-
-def place(r, q):
-    return 3 if q == side_of(r) else (main_of(r)[:1] + turned_of(r) + main_of(r)[1:]).index(q)
 
 
 def tile_ckconv_pa_kernel(tc, x, h_sine, w3, b3, bias, out):
@@ -198,7 +194,9 @@ def tile_ckconv_pa_kernel(tc, x, h_sine, w3, b3, bias, out):
             xs[r] = cod.tile([P, 512], U8, name="xs", tag="xs", bufs=5, align_bytes=256)
             quant(xc[r][:], xs[r][:], gx[r][:])
 
-        kb, ga, gb, kc, ks, kf = {}, {}, {}, {}, {}, {}
+        kb, kf, kt = {}, {}, {}
+        ga, gb, gs = {}, {}, {}
+        code_of = {}
 
         def stage1(r, q):
             g, n = q // 2, q % 2
@@ -218,11 +216,9 @@ def tile_ckconv_pa_kernel(tc, x, h_sine, w3, b3, bias, out):
             if q == side_of(r):
                 kf[r] = grp.tile([P, P, 4], F32, name="kf", tag="kf", bufs=2)
                 nc.scalar.copy(out=kf[r][:], in_=kb[r, q][:].rearrange("p t o -> p o t"))
-                flush()
 
-        kt = {}
-
-        def stage1_turned(r, q):
+        def stage1_turned(r):
+            q = turned_of(r)
             bank = tps.tile([P, 2, 2, P], F32, name="tbank", tag="tbank")
             n, c = q % 2, 512 * (q // 2)
             nc.tensor.matmul_mx(
@@ -238,53 +234,67 @@ def tile_ckconv_pa_kernel(tc, x, h_sine, w3, b3, bias, out):
             i = 2 * r + n
             nc.scalar.activation(out=kt[r][:], in_=bank[:].rearrange("o u e p -> o u p e"), func=IDENTITY, bias=b3T[:, i : i + 1], scale=1.0)
 
+        def even_banks(r):
+            if r not in ga:
+                ga[r] = grp.tile([P, 2, P, 4], BF16, name="ga", tag="ga", bufs=2, align_bytes=64)
+            return ga[r]
+
+        def pair_banks(r):
+            if r // 2 not in gb:
+                gb[r // 2] = grp.tile([P, 4, P, 4], BF16, name="gb", tag="gb", bufs=2, align_bytes=64)
+            return gb[r // 2]
+
         def flip_k(r):
             src = kt[r][:].rearrange("o u p e -> o (u p e)").bitcast(F32)
-            ga[r] = grp.tile([P, 2, P, 4], BF16, name="ga", tag="ga", bufs=3, align_bytes=64)
-            dest = ga[r][:, 1, :, :].rearrange("p o t -> p (o t)").bitcast(F32)
-            flip([(src, 0)], dest, "s")
+            flip([(src, 0)], pair_banks(r)[:, 1, :, :].rearrange("p o t -> p (o t)").bitcast(F32), "s")
 
         def b3_of(r, q):
             return b3bc[:, 2 * r + q % 2, :].unsqueeze(2).to_broadcast([P, P, 4])
 
-        gt = {}
+        def add_b3(r, q, dest, o0=0, o1=P):
+            nc.vector.tensor_tensor(out=dest[:, o0:o1, :], in0=kb[r, q][:, :, o0:o1].rearrange("p t o -> p o t"), in1=b3_of(r, q)[:, o0:o1, :], op=ADD)
 
-        def add_b3(r, q, o0=0, o1=P):
-            k = place(r, q)
-            if r not in ga:
-                ga[r] = grp.tile([P, 2, P, 4], BF16, name="ga", tag="ga", bufs=3, align_bytes=64)
-            if k == 2 and r not in gt:
-                gt[r] = grp.tile([P, P, 4], BF16, name="gt", tag="gt", bufs=3, align_bytes=64)
-            dest = ga[r][:, k, o0:o1, :] if k < 2 else gt[r][:, o0:o1, :]
-            nc.vector.tensor_tensor(out=dest, in0=kb[r, q][:, :, o0:o1].rearrange("p t o -> p o t"), in1=b3_of(r, q)[:, o0:o1, :], op=ADD)
+        def add_main(r):
+            for j, q in enumerate(main_of(r)):
+                add_b3(r, q, even_banks(r)[:, j, :, :] if r % 2 == 0 else pair_banks(r)[:, 2 + j, :, :])
+
+        def add_third(r, o0, o1):
+            add_b3(r, third_of(r), pair_banks(r)[:, 0, :, :], o0, o1)
 
         def side_add(r):
-            gb[r] = grp.tile([P, P, 4], BF16, name="gb", tag="gb", bufs=1, align_bytes=64)
-            nc.gpsimd.tensor_tensor(out=gb[r][:], in0=kf[r][:], in1=b3_of(r, side_of(r)), op=ADD)
+            gs[r] = grp.tile([P, P, 4], BF16, name="gs", tag="gs", bufs=1, align_bytes=64)
+            nc.gpsimd.tensor_tensor(out=gs[r][:], in0=kf[r][:], in1=b3_of(r, side_of(r)), op=ADD)
 
-        def quant_k(r, part):
-            if r not in kc:
-                kc[r] = cod.tile([P, 512], U32, name="kc", tag="kc", bufs=5, align_bytes=256)
-                ks[r] = cod.tile([P, 512], U8, name="ks", tag="ks", bufs=5, align_bytes=256)
-            if part == "a":
-                quant(kc[r][:, 0:256], ks[r][:, 0:256], ga[r][:].rearrange("p j o t -> p (j o t)"))
-            elif part == "b":
-                quant(kc[r][:, 256:384], ks[r][:, 256:384], gt[r][:].rearrange("p o t -> p (o t)"))
-            else:
-                quant(kc[r][:, 384:512], ks[r][:, 384:512], gb[r][:].rearrange("p o t -> p (o t)"))
+        def quant_banks(banks, src, tag, bufs):
+            n = len(banks)
+            codes = cod.tile([P, P * n], U32, name=tag, tag=tag, bufs=bufs, align_bytes=256)
+            scales = cod.tile([P, P * n], U8, name=tag + "s", tag=tag + "s", bufs=bufs, align_bytes=256)
+            quant(codes[:], scales[:], src)
+            for j, bank in enumerate(banks):
+                code_of[bank] = (codes[:, P * j : P * (j + 1)], scales[:, P * j : P * (j + 1)])
 
-        def stage2(r, banks):
+        def quant_side(r):
+            quant_banks([(r, side_of(r))], gs[r][:].rearrange("p o t -> p (o t)"), "cs", 6)
+
+        def quant_even(r):
+            quant_banks([(r, q) for q in main_of(r)], ga[r][:].rearrange("p j o t -> p (j o t)"), "ca", 4)
+
+        def quant_pair(r, j0=0, j1=4):
+            banks = [(r - 1, third_of(r - 1)), (r, turned_of(r))] + [(r, q) for q in main_of(r)]
+            quant_banks(banks[j0:j1], gb[r // 2][:, j0:j1, :, :].rearrange("p j o t -> p (j o t)"), "cb%d" % (j1 - j0), 4 if j1 - j0 == 4 else 2)
+
+        def stage2(r, banks, stop=False):
             for q in banks:
                 cols = slice(P * q, P * (q + 1))
-                kcols = slice(P * place(r, q), P * (place(r, q) + 1))
+                codes, scales = code_of[r, q]
                 nc.tensor.matmul_mx(
                     out=acc[:],
                     lhsT=xc[r][:, cols].bitcast(FP8X4),
                     lhsT_scale=xs[r][:, cols],
-                    rhs=kc[r][:, kcols].bitcast(FP8X4),
-                    rhs_scale=ks[r][:, kcols],
-                    start=(r == 0 and q == banks[0]),
-                    stop=(r == ROUNDS - 1 and q == banks[-1]),
+                    rhs=codes.bitcast(FP8X4),
+                    rhs_scale=scales,
+                    start=(r == 0 and q == 0),
+                    stop=(stop and q == banks[-1]),
                 )
 
         for k in range(12):
@@ -311,55 +321,52 @@ def tile_ckconv_pa_kernel(tc, x, h_sine, w3, b3, bias, out):
         side_add(0)
         stage1(0, 2)
         stage1(0, 3)
-        for q in turned_of(1):
-            stage1_turned(1, q)
+        stage1_turned(1)
 
         for s in range(ROUNDS):
-            nxt = s + 1 < ROUNDS
+            odd = s % 2 == 1
             last = s == ROUNDS - 1
             if last:
                 for r in x_turned(s - 2):
                     quant_x(r)
-            if s > 0 and has_third(s - 1):
-                add_b3(s - 1, main_of(s - 1)[2], P // 2, P)
-            for q in main_of(s)[:2]:
-                add_b3(s, q)
-            if has_third(s):
-                add_b3(s, main_of(s)[2], 0, P // 2)
-            if nxt:
-                main = main_of(s + 1)
-                stage1(s + 1, main[0])
+            if odd:
+                add_third(s - 1, P // 2, P)
+            add_main(s)
+            if not odd:
+                add_third(s, 0, P // 2)
+            if not last:
+                stage1(s + 1, main_of(s + 1)[0])
                 stage1(s + 1, side_of(s + 1))
-                for q in main[1:]:
-                    stage1(s + 1, q)
+                stage1(s + 1, main_of(s + 1)[1])
+                if odd:
+                    stage1(s + 1, third_of(s + 1))
             for r in products(s):
-                stage2(r, [q for q in [0, 1, 2, 3] if not (last and r == s - 1 and q == main_of(r)[2])])
+                stage2(r, [0, 1, 3] if last and r == s - 1 else [0, 1, 2, 3])
             if last:
-                quant_k(s, "a")
-                quant_k(s - 1, "b")
                 for r in x_turned(s - 1):
                     quant_x(r)
-                quant_k(s, "b")
-                quant_k(s, "s")
-                stage2(s - 1, [main_of(s - 1)[2]])
-                stage2(s, [0, 2, 1, 3])
+                quant_pair(s, 2, 4)
+                quant_pair(s, 0, 2)
+                quant_side(s)
+                stage2(s, [0, 1])
+                stage2(s - 1, [2])
+                stage2(s, [2, 3], True)
                 break
             if s + 2 < ROUNDS:
                 quant_w(s + 2)
-            for q in turned_of(s + 2) if s + 2 < ROUNDS else []:
-                stage1_turned(s + 2, q)
+            if s % 2 == 1 and s + 2 < ROUNDS:
+                stage1_turned(s + 2)
             for r in x_turned(s - 2):
                 quant_x(r)
-            if s > 0 and has_third(s - 1):
-                quant_k(s - 1, "b")
-            if not has_third(s):
-                quant_k(s, "b")
-            quant_k(s, "s")
-            quant_k(s, "a")
+            quant_side(s)
+            if odd:
+                quant_pair(s)
+            else:
+                quant_even(s)
             side_add(s + 1)
             if s + 3 < ROUNDS:
                 flip_w(s + 3)
-            if turned_of(s + 1):
+            if not odd:
                 flip_k(s + 1)
             for r in x_turned(s):
                 flip_x(r)

@@ -60,9 +60,9 @@ def tile_ckconv_pa_kernel(tc, x, h_sine, w3, b3, bias, out):
         hs_view = h_sine.rearrange("(g u p e) h -> g p u (e h)", g=2, u=2, p=P, e=2)
         w_view = w3.rearrange("(o i) h -> o (i h)", i=CIN)
         x_view = x.rearrange("b i l -> b (i l)")
-        hs_sb = [const.tile([P, 1024], BF16, name="hs_sb%d" % k) for k in range(4)]
-        w_sb = [loads.tile([P, 1024], BF16, name="w_sb%d" % r) for r in range(ROUNDS)]
-        x_sb = [loads.tile([P, 2048], BF16, name="x_sb%d" % r) for r in range(ROUNDS)]
+        hs_sb = [const.tile([P, 1024], BF16, name="hs_sb%d" % k, align_bytes=256) for k in range(4)]
+        w_sb = [loads.tile([P, 1024], BF16, name="w_sb%d" % r, align_bytes=256) for r in range(ROUNDS)]
+        x_sb = [loads.tile([P, 2048], BF16, name="x_sb%d" % r, align_bytes=256) for r in range(ROUNDS)]
 
         def load_w(r):
             nc.sync.dma_start(out=w_sb[r][:], in_=w_view[:, 1024 * r : 1024 * (r + 1)])
@@ -77,7 +77,7 @@ def tile_ckconv_pa_kernel(tc, x, h_sine, w3, b3, bias, out):
 
         zeros = const.tile([P, P], BF16, name="zeros")
         nc.gpsimd.memset(zeros[:], 0.0)
-        ident_f = const.tile([P, P], F32, name="ident_f")
+        ident_f = const.tile([P, P], F32, name="ident_f", align_bytes=256)
         ident_b = const.tile([P, P], BF16, name="ident_b")
         make_identity(nc, ident_b[:])
         make_identity(nc, ident_f[:])
@@ -101,7 +101,7 @@ def tile_ckconv_pa_kernel(tc, x, h_sine, w3, b3, bias, out):
 
         for r in range(5):
             load_round(r)
-        b3bc = const.tile([P, CIN, P], BF16, name="b3bc")
+        b3bc = const.tile([P, CIN, P], BF16, name="b3bc", align_bytes=256)
         hs_codes = const.tile([P, 1024], U32, name="hs_codes", align_bytes=256)
         hs_scales = const.tile([P, 1024], U8, name="hs_scales", align_bytes=256)
         acc = aps.tile([P, P], F32, name="acc")
@@ -154,7 +154,7 @@ def tile_ckconv_pa_kernel(tc, x, h_sine, w3, b3, bias, out):
 
         def flip_h(g, half, engine):
             if half == 0:
-                gh[g] = grp.tile([P, 2048], BF16, name="gh", tag="gh", bufs=2, align_bytes=64)
+                gh[g] = grp.tile([P, 2048], BF16, name="gh", tag="gh", bufs=2, align_bytes=256)
             src = hs_sb[2 * g + half][:].bitcast(F32)
             flip([(src, 0), (src, 256)], gh[g][:].bitcast(F32)[:, 512 * half : 512 * (half + 1)], engine)
 
@@ -168,7 +168,7 @@ def tile_ckconv_pa_kernel(tc, x, h_sine, w3, b3, bias, out):
         gw, wc, ws = {}, {}, {}
 
         def flip_w(r):
-            gw[r] = grp.tile([P, 1024], BF16, name="gw", tag="gw", align_bytes=64)
+            gw[r] = grp.tile([P, 1024], BF16, name="gw", tag="gw", align_bytes=256)
             src = w_sb[r][:].bitcast(F32)
             flip([(src, 0), (src, 256)], gw[r][:].bitcast(F32), "s")
 
@@ -181,7 +181,7 @@ def tile_ckconv_pa_kernel(tc, x, h_sine, w3, b3, bias, out):
 
         def flip_x_half(r, g, later=False):
             if g == 0:
-                gx[r] = grp.tile([P, 2048], BF16, name="gx", tag="gx", bufs=4, align_bytes=64)
+                gx[r] = grp.tile([P, 2048], BF16, name="gx", tag="gx", bufs=4, align_bytes=256)
             src = x_sb[r][:].bitcast(F32)
             flip([(src, 256 * g), (src, 512 + 256 * g)], gx[r][:].bitcast(F32)[:, 512 * g : 512 * (g + 1)], "s", later)
 
@@ -214,7 +214,7 @@ def tile_ckconv_pa_kernel(tc, x, h_sine, w3, b3, bias, out):
                     stop=True,
                 )
             if q == side_of(r):
-                kf[r] = grp.tile([P, P, 4], F32, name="kf", tag="kf", bufs=2)
+                kf[r] = grp.tile([P, P, 4], F32, name="kf", tag="kf", bufs=2, align_bytes=256)
                 nc.scalar.copy(out=kf[r][:], in_=kb[r, q][:].rearrange("p t o -> p o t"))
 
         def stage1_turned(r):
@@ -230,18 +230,18 @@ def tile_ckconv_pa_kernel(tc, x, h_sine, w3, b3, bias, out):
                 start=True,
                 stop=True,
             )
-            kt[r] = grp.tile([P, 2, P, 2], BF16, name="kt", tag="kt", bufs=2)
+            kt[r] = grp.tile([P, 2, P, 2], BF16, name="kt", tag="kt", bufs=2, align_bytes=256)
             i = 2 * r + n
             nc.scalar.activation(out=kt[r][:], in_=bank[:].rearrange("o u e p -> o u p e"), func=IDENTITY, bias=b3T[:, i : i + 1], scale=1.0)
 
         def even_banks(r):
             if r not in ga:
-                ga[r] = grp.tile([P, 2, P, 4], BF16, name="ga", tag="ga", bufs=2, align_bytes=64)
+                ga[r] = grp.tile([P, 2, P, 4], BF16, name="ga", tag="ga", bufs=2, align_bytes=256)
             return ga[r]
 
         def pair_banks(r):
             if r // 2 not in gb:
-                gb[r // 2] = grp.tile([P, 4, P, 4], BF16, name="gb", tag="gb", bufs=2, align_bytes=64)
+                gb[r // 2] = grp.tile([P, 4, P, 4], BF16, name="gb", tag="gb", bufs=2, align_bytes=256)
             return gb[r // 2]
 
         def flip_k(r):
@@ -262,7 +262,7 @@ def tile_ckconv_pa_kernel(tc, x, h_sine, w3, b3, bias, out):
             add_b3(r, third_of(r), pair_banks(r)[:, 0, :, :], o0, o1)
 
         def side_add(r):
-            gs[r] = grp.tile([P, P, 4], BF16, name="gs", tag="gs", bufs=1, align_bytes=64)
+            gs[r] = grp.tile([P, P, 4], BF16, name="gs", tag="gs", bufs=1, align_bytes=256)
             nc.gpsimd.tensor_tensor(out=gs[r][:], in0=kf[r][:], in1=b3_of(r, side_of(r)), op=ADD)
 
         def quant_banks(banks, src, tag, bufs):

from contextlib import ExitStack

import concourse.mybir as mybir
from concourse.masks import make_identity

F32 = mybir.dt.float32
BF16 = mybir.dt.bfloat16
U32 = mybir.dt.uint32
U8 = mybir.dt.uint8
FP8X4 = mybir.dt.float8_e4m3fn_x4
ADD = mybir.AluOpType.add
IDENTITY = mybir.ActivationFunctionType.Identity

P = 128
CIN = 32
ROUNDS = 16
FLOPS = 2 * 1024 * 4096 * 512 + 2 * 128 * 128 * 32768


def main_of(r):
    return [0, 2] if r == 0 else [0, 1]


def third_of(r):
    return 3 if r == 0 else 2


def turned_of(r):
    return 2


def side_of(r):
    return 1 if r == 0 else 3


def x_turned(s):
    if s < 0 or s == ROUNDS - 1:
        return []
    return [s] if s < ROUNDS - 3 else [s, s + 1] if s == ROUNDS - 3 else [s + 1]


def products(s):
    return [s - 3] if 3 <= s < ROUNDS - 1 else [s - 3, s - 2, s - 1] if s == ROUNDS - 1 else []


def tile_ckconv_pa_kernel(tc, x, h_sine, w3, b3, bias, out):
    nc = tc.nc
    with ExitStack() as ctx:
        ctx.enter_context(tc.manual_schedule())
        const = ctx.enter_context(tc.tile_pool(name="const", bufs=1))
        loads = ctx.enter_context(tc.tile_pool(name="loads", bufs=1))
        grp = ctx.enter_context(tc.tile_pool(name="grp", bufs=3))
        cod = ctx.enter_context(tc.tile_pool(name="cod", bufs=3))
        tps = ctx.enter_context(tc.psum_pool(name="ps_t", bufs=4))
        kps = ctx.enter_context(tc.psum_pool(name="ps_k", bufs=3))
        aps = ctx.enter_context(tc.psum_pool(name="ps_a", bufs=1))

        b3T = const.tile([P, CIN], BF16, name="b3T")
        nc.sync.dma_start(out=b3T[:], in_=b3.rearrange("(o i) -> o i", i=CIN))
        hs_view = h_sine.rearrange("(g u p e) h -> g p u (e h)", g=2, u=2, p=P, e=2)
        w_view = w3.rearrange("(o i) h -> o (i h)", i=CIN)
        x_view = x.rearrange("b i l -> b (i l)")
        hs_sb = [const.tile([P, 1024], BF16, name="hs_sb%d" % k, align_bytes=256) for k in range(4)]
        w_sb = [loads.tile([P, 1024], BF16, name="w_sb%d" % r, align_bytes=256) for r in range(ROUNDS)]
        x_sb = [loads.tile([P, 2048], BF16, name="x_sb%d" % r, align_bytes=256) for r in range(ROUNDS)]

        def load_w(r):
            nc.sync.dma_start(out=w_sb[r][:], in_=w_view[:, 1024 * r : 1024 * (r + 1)])

        def load_x(r):
            nc.sync.dma_start(out=x_sb[r][:], in_=x_view[:, 2048 * r : 2048 * (r + 1)])

        def load_h(g):
            for u in range(2):
                nc.sync.dma_start(out=hs_sb[2 * g + u][:], in_=hs_view[g][:, u, :])


        zeros = const.tile([P, P], BF16, name="zeros")
        nc.gpsimd.memset(zeros[:], 0.0)
        ident_f = const.tile([P, P], F32, name="ident_f", align_bytes=256)
        ident_b = const.tile([P, P], BF16, name="ident_b")
        make_identity(nc, ident_b[:])
        make_identity(nc, ident_f[:])

        b3T4 = const.tile([P, 4, CIN], BF16, name="b3T4")
        b3rows = const.tile([P, P], BF16, name="b3rows")
        scratch = out.rearrange("b o z -> (b o z)")[0 : CIN * P // 2]

        bias_bc = const.tile([P, P], BF16, name="bias_bc")
        load_h(0)
        load_w(0)
        load_h(1)
        load_w(1)
        load_w(2)
        nc.sync.dma_start(out=b3T4[:], in_=b3.rearrange("(o i) -> o i", i=CIN).unsqueeze(1).to_broadcast([P, 4, CIN]))

        def load_round(r):
            if r + 3 < ROUNDS:
                load_w(r + 3)
            load_x(r)

        for r in range(5):
            load_round(r)
        b3bc = const.tile([P, CIN, P], BF16, name="b3bc", align_bytes=256)
        hs_codes = const.tile([P, 1024], U32, name="hs_codes", align_bytes=256)
        hs_scales = const.tile([P, 1024], U8, name="hs_scales", align_bytes=256)
        acc = aps.tile([P, P], F32, name="acc")

        def leave(engine, dest, src):
            if engine == "v":
                nc.vector.tensor_copy(out=dest, in_=src)
            else:
                nc.scalar.copy(out=dest, in_=src)

        waiting = {"copies": []}

        def flush():
            for engine, dest, src in waiting["copies"]:
                leave(engine, dest, src)
            waiting["copies"] = []

        def flip(units, dest, engine, later=False):
            bank = tps.tile([P, len(units), 2, P], F32, name="tbank", tag="tbank")
            for n, (src, col) in enumerate(units):
                for u in range(2):
                    nc.tensor.transpose(bank[:, n, u, :], src[:, col + P * u : col + P * (u + 1)], ident_f[:])
            waiting["copies"].append((engine, dest.rearrange("p (n r u) -> p n r u", r=P, u=2), bank[:].rearrange("p n u r -> p n r u")))
            if not later:
                flush()

        def spread_b3(jb, engine):
            bank = tps.tile([P, 8, P], BF16, name="bbank", tag="tbank")
            for q in range(8):
                c = 8 * jb + q
                nc.tensor.matmul(out=bank[:, q, :], lhsT=b3T[:, c : c + 1].to_broadcast([P, P]), rhs=ident_b[:], start=True, stop=True)
            leave(engine, b3bc[:, 8 * jb : 8 * (jb + 1), :], bank[:])

        def park_b3():
            bank = tps.tile([P, P], BF16, name="rbank", tag="tbank")
            nc.tensor.transpose(bank[:], b3T4[:].rearrange("p k i -> p (k i)"), ident_b[:])
            nc.scalar.copy(out=b3rows[:], in_=bank[:])
            nc.sync.dma_start(out=scratch.rearrange("(i w) -> i w", i=CIN), in_=b3rows[0:CIN, :].bitcast(F32))
            for r in range(5, 7):
                load_round(r)
            nc.sync.dma_start(
                out=b3bc[:, 16:CIN, :].rearrange("p i o -> p (i o)").bitcast(F32),
                in_=scratch[16 * P // 2 :].partition_broadcast(P),
            )
            for r in range(7, ROUNDS):
                load_round(r)
            nc.sync.dma_start(out=bias_bc[:], in_=bias.partition_broadcast(P))

        gh = {}

        def flip_h(g, half, engine):
            if half == 0:
                gh[g] = grp.tile([P, 2048], BF16, name="gh", tag="gh", bufs=2, align_bytes=256)
            src = hs_sb[2 * g + half][:].bitcast(F32)
            flip([(src, 0), (src, 256)], gh[g][:].bitcast(F32)[:, 512 * half : 512 * (half + 1)], engine)

        def quant(codes, scales, src):
            nc.vector.quantize_mx(out=codes.bitcast(FP8X4), scales=scales, in_=src)

        def quant_h(g, half):
            c = 512 * g + 256 * half
            quant(hs_codes[:, c : c + 256], hs_scales[:, c : c + 256], gh[g][:, 1024 * half : 1024 * (half + 1)])

        gw, wc, ws = {}, {}, {}

        def flip_w(r):
            gw[r] = grp.tile([P, 1024], BF16, name="gw", tag="gw", align_bytes=256)
            src = w_sb[r][:].bitcast(F32)
            flip([(src, 0), (src, 256)], gw[r][:].bitcast(F32), "s")

        def quant_w(r):
            wc[r] = cod.tile([P, 256], U32, name="wc", tag="wc", align_bytes=256)
            ws[r] = cod.tile([P, 256], U8, name="ws", tag="ws", align_bytes=256)
            quant(wc[r][:], ws[r][:], gw[r][:])

        gx, xc, xs = {}, {}, {}

        def flip_x_half(r, g, later=False):
            if g == 0:
                gx[r] = grp.tile([P, 2048], BF16, name="gx", tag="gx", bufs=4, align_bytes=256)
            src = x_sb[r][:].bitcast(F32)
            flip([(src, 256 * g), (src, 512 + 256 * g)], gx[r][:].bitcast(F32)[:, 512 * g : 512 * (g + 1)], "s", later)

        def flip_x(r):
            flip_x_half(r, 0)
            flip_x_half(r, 1)

        def quant_x(r):
            xc[r] = cod.tile([P, 512], U32, name="xc", tag="xc", bufs=5, align_bytes=256)
            xs[r] = cod.tile([P, 512], U8, name="xs", tag="xs", bufs=5, align_bytes=256)
            quant(xc[r][:], xs[r][:], gx[r][:])

        kb, kf, kt = {}, {}, {}
        ga, gb, gs = {}, {}, {}
        code_of = {}

        def stage1(r, q):
            g, n = q // 2, q % 2
            pool, tag = (tps, "tbank") if q == side_of(r) else (kps, "kbank")
            kb[r, q] = pool.tile([P, 4, P], F32, name="kbank", tag=tag)
            for t in range(4):
                c = P * (4 * g + t)
                nc.tensor.matmul_mx(
                    out=kb[r, q][:, t, :],
                    lhsT=hs_codes[:, c : c + P].bitcast(FP8X4),
                    lhsT_scale=hs_scales[:, c : c + P],
                    rhs=wc[r][:, P * n : P * (n + 1)].bitcast(FP8X4),
                    rhs_scale=ws[r][:, P * n : P * (n + 1)],
                    start=True,
                    stop=True,
                )
            if q == side_of(r):
                kf[r] = grp.tile([P, P, 4], F32, name="kf", tag="kf", bufs=2, align_bytes=256)
                nc.scalar.copy(out=kf[r][:], in_=kb[r, q][:].rearrange("p t o -> p o t"))

        def stage1_turned(r):
            q = turned_of(r)
            bank = tps.tile([P, 2, 2, P], F32, name="tbank", tag="tbank")
            n, c = q % 2, 512 * (q // 2)
            nc.tensor.matmul_mx(
                out=bank[:].rearrange("o u e p -> o (u e p)"),
                lhsT=wc[r][:, P * n : P * (n + 1)].bitcast(FP8X4),
                lhsT_scale=ws[r][:, P * n : P * (n + 1)],
                rhs=hs_codes[:, c : c + 512].bitcast(FP8X4),
                rhs_scale=hs_scales[:, c : c + 512],
                start=True,
                stop=True,
            )
            kt[r] = grp.tile([P, 2, P, 2], BF16, name="kt", tag="kt", bufs=2, align_bytes=256)
            i = 2 * r + n
            nc.scalar.activation(out=kt[r][:], in_=bank[:].rearrange("o u e p -> o u p e"), func=IDENTITY, bias=b3T[:, i : i + 1], scale=1.0)

        def even_banks(r):
            if r not in ga:
                ga[r] = grp.tile([P, 2, P, 4], BF16, name="ga", tag="ga", bufs=2, align_bytes=256)
            return ga[r]

        def pair_banks(r):
            if r // 2 not in gb:
                gb[r // 2] = grp.tile([P, 4, P, 4], BF16, name="gb", tag="gb", bufs=2, align_bytes=256)
            return gb[r // 2]

        def flip_k(r):
            src = kt[r][:].rearrange("o u p e -> o (u p e)").bitcast(F32)
            flip([(src, 0)], pair_banks(r)[:, 1, :, :].rearrange("p o t -> p (o t)").bitcast(F32), "s")

        def b3_of(r, q):
            return b3bc[:, 2 * r + q % 2, :].unsqueeze(2).to_broadcast([P, P, 4])

        def add_b3(r, q, dest, o0=0, o1=P):
            nc.vector.tensor_tensor(out=dest[:, o0:o1, :], in0=kb[r, q][:, :, o0:o1].rearrange("p t o -> p o t"), in1=b3_of(r, q)[:, o0:o1, :], op=ADD)

        def add_main(r):
            for j, q in enumerate(main_of(r)):
                add_b3(r, q, even_banks(r)[:, j, :, :] if r % 2 == 0 else pair_banks(r)[:, 2 + j, :, :])

        def add_third(r, o0, o1):
            add_b3(r, third_of(r), pair_banks(r)[:, 0, :, :], o0, o1)

        def side_add(r):
            gs[r] = grp.tile([P, P, 4], BF16, name="gs", tag="gs", bufs=1, align_bytes=256)
            nc.gpsimd.tensor_tensor(out=gs[r][:], in0=kf[r][:], in1=b3_of(r, side_of(r)), op=ADD)

        def quant_banks(banks, src, tag, bufs):
            n = len(banks)
            codes = cod.tile([P, P * n], U32, name=tag, tag=tag, bufs=bufs, align_bytes=256)
            scales = cod.tile([P, P * n], U8, name=tag + "s", tag=tag + "s", bufs=bufs, align_bytes=256)
            quant(codes[:], scales[:], src)
            for j, bank in enumerate(banks):
                code_of[bank] = (codes[:, P * j : P * (j + 1)], scales[:, P * j : P * (j + 1)])

        def quant_side(r):
            quant_banks([(r, side_of(r))], gs[r][:].rearrange("p o t -> p (o t)"), "cs", 6)

        def quant_even(r):
            quant_banks([(r, q) for q in main_of(r)], ga[r][:].rearrange("p j o t -> p (j o t)"), "ca", 4)

        def quant_pair(r, j0=0, j1=4):
            banks = [(r - 1, third_of(r - 1)), (r, turned_of(r))] + [(r, q) for q in main_of(r)]
            quant_banks(banks[j0:j1], gb[r // 2][:, j0:j1, :, :].rearrange("p j o t -> p (j o t)"), "cb%d" % (j1 - j0), 4 if j1 - j0 == 4 else 2)

        def stage2(r, banks, stop=False):
            for q in banks:
                cols = slice(P * q, P * (q + 1))
                codes, scales = code_of[r, q]
                nc.tensor.matmul_mx(
                    out=acc[:],
                    lhsT=xc[r][:, cols].bitcast(FP8X4),
                    lhsT_scale=xs[r][:, cols],
                    rhs=codes.bitcast(FP8X4),
                    rhs_scale=scales,
                    start=(r == 0 and q == 0),
                    stop=(stop and q == banks[-1]),
                )

        for k in range(12):
            nc.tensor.matmul(out=acc[:], lhsT=zeros[:], rhs=zeros[:], start=True, stop=True)

        spread_b3(0, "v")
        flip_h(0, 0, "s")
        flip_h(0, 1, "v")
        quant_h(0, 0)
        quant_h(0, 1)
        flip_w(0)
        spread_b3(1, "s")
        quant_w(0)
        flip_h(1, 0, "s")
        flip_h(1, 1, "v")
        flip_w(1)
        stage1(0, 0)
        stage1(0, 1)
        flip_w(2)
        park_b3()
        quant_h(1, 0)
        quant_h(1, 1)
        quant_w(1)
        side_add(0)
        stage1(0, 2)
        stage1(0, 3)
        stage1_turned(1)

        for s in range(ROUNDS):
            odd = s % 2 == 1
            last = s == ROUNDS - 1
            if last:
                for r in x_turned(s - 2):
                    quant_x(r)
            if odd:
                add_third(s - 1, P // 2, P)
            add_main(s)
            if not odd:
                add_third(s, 0, P // 2)
            if not last:
                stage1(s + 1, main_of(s + 1)[0])
                stage1(s + 1, side_of(s + 1))
                stage1(s + 1, main_of(s + 1)[1])
                if odd:
                    stage1(s + 1, third_of(s + 1))
            for r in products(s):
                stage2(r, [0, 1, 3] if last and r == s - 1 else [0, 1, 2, 3])
            if last:
                for r in x_turned(s - 1):
                    quant_x(r)
                quant_pair(s, 2, 4)
                quant_pair(s, 0, 2)
                quant_side(s)
                stage2(s, [0, 1])
                stage2(s - 1, [2])
                stage2(s, [2, 3], True)
                break
            if s + 2 < ROUNDS:
                quant_w(s + 2)
            if s % 2 == 1 and s + 2 < ROUNDS:
                stage1_turned(s + 2)
            for r in x_turned(s - 2):
                quant_x(r)
            quant_side(s)
            if odd:
                quant_pair(s)
            else:
                quant_even(s)
            side_add(s + 1)
            if s + 3 < ROUNDS:
                flip_w(s + 3)
            if not odd:
                flip_k(s + 1)
            for r in x_turned(s):
                flip_x(r)

        res = const.tile([P, P], F32, name="res")
        nc.vector.tensor_tensor(out=res[:], in0=acc[:], in1=bias_bc[:], op=ADD)
        nc.sync.dma_start(out=out.rearrange("b o z -> b (o z)"), in_=res[:])
